import numpy as np
import ml_dtypes


def mxq(x, axis, fmt="e4m3"):
    dtype, down = {"e4m3": (ml_dtypes.float8_e4m3fn, 7), "e5m2": (ml_dtypes.float8_e5m2, 14)}[fmt]
    v = np.moveaxis(np.asarray(x, np.float32).astype(ml_dtypes.bfloat16).astype(np.float64), axis, -1)
    blocks = v.reshape(v.shape[:-1] + (-1, 32))
    amax = np.abs(blocks).max(-1, keepdims=True)
    byte = np.maximum(np.where(amax > 0, np.frexp(amax)[1] - 1 + 127, 0) - down, 1)
    scale = np.exp2(byte - 127.0)
    codes = (blocks / scale).astype(np.float32).astype(dtype).astype(np.float64)
    return np.moveaxis((codes * scale).reshape(v.shape), -1, axis)


WIDE = False


def mx_kscale(k):
    if not WIDE:
        return np.ones(k)
    levels = np.array([10, -10, 5, -5, 0])
    a = np.random.permutation(np.resize(levels, k // 512 * 4)).reshape(k // 512, 4)
    idx = np.arange(k)
    return np.exp2(a[idx // 512, idx % 128 // 32])


BF16 = ml_dtypes.bfloat16


def bf(x):
    return np.asarray(x, np.float32).astype(BF16)


def f64(x):
    return np.asarray(x).astype(np.float64)


B, N, F, U, S = 2, 2048, 128, 128, 2
C = S * (F + U)


def sigmoid(v):
    return 1.0 / (1.0 + np.exp(-v))


def random_walk():
    a = np.random.uniform(size=(N, N))
    return a / a.sum(axis=1, keepdims=True) * np.sqrt(N)


def setup_inputs():
    s = mx_kscale(N)
    return {"r_prev": bf(sigmoid(np.random.standard_normal((B, U, N))) * np.random.standard_normal((B, U, N)) * s),
            "h_diff": bf(np.random.standard_normal((B, N, S * F))),
            "u": bf(sigmoid(np.random.standard_normal((B, N, U)))),
            "state": bf(np.random.standard_normal((B, U * N))),
            "support0": bf(random_walk() / s[None, :]),
            "support1": bf(random_walk() / s[None, :]),
            "c_kernel": bf(np.random.standard_normal((C, U)) / np.sqrt(C))}


def diffuse(xq, supq):
    return np.concatenate([(xq @ sq.T) for sq in supq], axis=1)


def reference(r_prev, h_diff, u, state, support0, support1, c_kernel):
    supq = (mxq(f64(support0), 1, "e4m3"), mxq(f64(support1), 1, "e4m3"))
    c_state = diffuse(mxq(f64(r_prev), 2, "e4m3"), supq).transpose(0, 2, 1)
    hc = np.concatenate([f64(h_diff), c_state], axis=-1)
    c = np.tanh(mxq(hc, 2, "e4m3") @ mxq(f64(c_kernel), 0, "e4m3"))
    prev_t = f64(state).reshape(B, U, N).transpose(0, 2, 1)
    ug = f64(u)
    z = ug * prev_t + (1.0 - ug) * c
    return z.reshape(B, U * N)

@@ -1,0 +1,243 @@
+from contextlib import ExitStack
+
+import concourse.mybir as mybir
+from concourse.masks import make_identity
+
+F32 = mybir.dt.float32
+BF16 = mybir.dt.bfloat16
+U32 = mybir.dt.uint32
+U8 = mybir.dt.uint8
+FP8X4 = mybir.dt.float8_e4m3fn_x4
+ALU = mybir.AluOpType
+TANH = mybir.ActivationFunctionType.Tanh
+
+P = 128
+BATCH = 2
+NODES = 2048
+UNITS = 128
+FEATS = 256
+SUPPORTS = 2
+PACK = 4
+K_PASS = P * PACK
+PASSES = NODES // K_PASS
+BANK = 512
+ROWS = 2
+ROUND = P * ROWS
+ROUNDS = NODES // ROUND
+STEPS = ROUNDS * ROWS
+AHEAD = 3
+
+FLOPS = 2 * SUPPORTS * BATCH * UNITS * NODES * NODES + 2 * BATCH * NODES * (FEATS + SUPPORTS * UNITS) * UNITS
+
+
+def transpose_512_words(nc, banks, identity, copy, words_in, words_out):
+    bank = banks.tile([P, BANK], F32, tag="bank")
+    for block in range(BANK // P):
+        cols = slice(block * P, (block + 1) * P)
+        nc.tensor.transpose(out=bank[:, cols], in_=words_in[:, cols], identity=identity)
+    copy(
+        out=words_out.rearrange("p (g r u) -> p g r u", g=2, u=2),
+        in_=bank[:].rearrange("p (g u r) -> p g r u", g=2, u=2),
+    )
+
+
+def tile_gcrnncell_pb_kernel(tc, r_prev, h_diff, u, state, support0, support1, c_kernel, out):
+    nc = tc.nc
+    supports = (support0, support1)
+    state_rows = state.rearrange("b (k n) -> k b n", n=NODES)
+    out_rows = out.rearrange("b (m k) -> b m k", k=UNITS)
+
+    with ExitStack() as stack:
+        keep = stack.enter_context(tc.tile_pool(name="keep", bufs=1))
+        big_in = stack.enter_context(tc.tile_pool(name="big_in", bufs=AHEAD))
+        small_in = stack.enter_context(tc.tile_pool(name="small_in", bufs=AHEAD + 1))
+        moving = stack.enter_context(tc.tile_pool(name="moving", bufs=4))
+        ending = stack.enter_context(tc.tile_pool(name="ending", bufs=2))
+        banks = stack.enter_context(tc.psum_pool(name="banks", bufs=3))
+        sums = stack.enter_context(tc.psum_pool(name="sums", bufs=3))
+        single = stack.enter_context(tc.psum_pool(name="single", bufs=1))
+
+        sup_raw = {}
+        h_raw = {}
+        u_raw = {}
+        state_raw = {}
+
+        def load_round(q):
+            rows = slice(q * ROUND, (q + 1) * ROUND)
+            for i in range(SUPPORTS):
+                sup_raw[q, i] = big_in.tile([P, ROWS * NODES], BF16, name="sup", tag="sup%d" % i)
+                nc.sync.dma_start(
+                    out=sup_raw[q, i][:], in_=supports[i][rows, :].rearrange("(p j) n -> p (j n)", j=ROWS)
+                )
+            h_raw[q] = small_in.tile([P, BATCH * ROWS * FEATS], BF16, name="h", tag="h")
+            nc.sync.dma_start(
+                out=h_raw[q][:].rearrange("p (b x) -> p b x", b=BATCH),
+                in_=h_diff[:, rows, :].rearrange("b (p j) c -> p b (j c)", j=ROWS),
+            )
+            state_raw[q] = small_in.tile([P, BATCH * ROUND], BF16, name="st", tag="st")
+            nc.sync.dma_start(
+                out=state_raw[q][:].rearrange("p (b n) -> p b n", b=BATCH), in_=state_rows[:, :, rows]
+            )
+            u_raw[q] = small_in.tile([P, BATCH * ROWS * UNITS], BF16, name="gate", tag="gate")
+            nc.sync.dma_start(
+                out=u_raw[q][:].rearrange("p (b x) -> p b x", b=BATCH),
+                in_=u[:, rows, :].rearrange("b (p j) k -> p b (j k)", j=ROWS),
+            )
+
+        r_raw = keep.tile([P, BATCH * NODES], BF16)
+        nc.sync.dma_start(
+            out=r_raw[:].rearrange("p (b n) -> p b n", b=BATCH), in_=r_prev.rearrange("b k n -> k b n")
+        )
+        ck_raw = keep.tile([P, PACK * UNITS], BF16)
+        nc.sync.dma_start(
+            out=ck_raw[:].rearrange("p (t k) -> p t k", t=PACK), in_=c_kernel.rearrange("(t p) k -> p t k", p=P)
+        )
+        for q in range(AHEAD):
+            load_round(q)
+
+        ident_f32 = keep.tile([P, P], F32)
+        make_identity(nc, ident_f32[:])
+        ident_bf16 = keep.tile([P, P], BF16)
+        make_identity(nc, ident_bf16[:])
+
+        r_grouped = keep.tile([P, BATCH * NODES], BF16, align_bytes=64)
+        r_codes = keep.tile([P, BATCH * PASSES * UNITS], U32, align_bytes=64)
+        r_scales = keep.tile([P, BATCH * PASSES * UNITS], U8, align_bytes=64)
+        for piece in range(BATCH * NODES // (2 * BANK)):
+            words = slice(piece * BANK, (piece + 1) * BANK)
+            transpose_512_words(
+                nc,
+                banks,
+                ident_f32[:],
+                nc.scalar.copy if piece % 2 == 0 else nc.vector.tensor_copy,
+                r_raw[:].bitcast(F32)[:, words],
+                r_grouped[:].bitcast(F32)[:, words],
+            )
+        nc.vector.quantize_mx(out=r_codes[:].bitcast(FP8X4), scales=r_scales[:], in_=r_grouped[:])
+
+        ck_grouped = keep.tile([P, UNITS * PACK], BF16, align_bytes=64)
+        ck_codes = keep.tile([P, UNITS], U32, align_bytes=64)
+        ck_scales = keep.tile([P, UNITS], U8, align_bytes=64)
+        nc.vector.tensor_copy(
+            out=ck_grouped[:].rearrange("p (k t) -> p k t", t=PACK),
+            in_=ck_raw[:].rearrange("p (t k) -> p k t", t=PACK),
+        )
+        nc.vector.quantize_mx(out=ck_codes[:].bitcast(FP8X4), scales=ck_scales[:], in_=ck_grouped[:])
+
+        sup_codes = {}
+        sup_scales = {}
+        hc_grouped = {}
+        prev_bank = {}
+
+        def quantise_supports(s):
+            q, j = divmod(s, ROWS)
+            for i in range(SUPPORTS):
+                grouped = moving.tile([P, PACK * BANK], BF16, align_bytes=64)
+                for half in range(2):
+                    transpose_512_words(
+                        nc,
+                        banks,
+                        ident_f32[:],
+                        nc.scalar.copy,
+                        sup_raw[q, i][:].bitcast(F32)[:, (2 * j + half) * BANK : (2 * j + half + 1) * BANK],
+                        grouped[:].bitcast(F32)[:, half * BANK : (half + 1) * BANK],
+                    )
+                sup_codes[s, i] = moving.tile([P, BANK], U32, name="codes", tag="codes", align_bytes=64)
+                sup_scales[s, i] = moving.tile([P, BANK], U8, name="scales", tag="scales", align_bytes=64)
+                nc.vector.quantize_mx(
+                    out=sup_codes[s, i][:].bitcast(FP8X4), scales=sup_scales[s, i][:], in_=grouped[:]
+                )
+
+        def transpose_state(q):
+            prev_bank[q] = single.tile([P, BATCH * UNITS], F32, name="prev", tag="prev")
+            for b in range(BATCH):
+                cols = slice(b * P, (b + 1) * P)
+                nc.tensor.transpose(
+                    out=prev_bank[q][:, cols], in_=state_raw[q][:].bitcast(F32)[:, cols], identity=ident_f32[:]
+                )
+
+        def diffuse(s):
+            q, j = divmod(s, ROWS)
+            if j == 0:
+                hc_grouped[q] = ending.tile([P, BATCH * ROWS * P * PACK], BF16, name="hc", tag="hc", align_bytes=64)
+            planes = []
+            for b in range(BATCH):
+                planes.append(sums.tile([P, BANK], F32, name="planes", tag="planes"))
+                for t in range(FEATS // P):
+                    first = (b * ROWS + j) * FEATS + t * P
+                    nc.tensor.matmul(
+                        out=planes[b][:, t * P : (t + 1) * P],
+                        lhsT=h_raw[q][:, first : first + P],
+                        rhs=ident_bf16[:],
+                        start=True,
+                        stop=True,
+                    )
+            for i in range(SUPPORTS):
+                for b in range(BATCH):
+                    for g in range(PASSES):
+                        units = slice((b * PASSES + g) * UNITS, (b * PASSES + g + 1) * UNITS)
+                        nodes = slice(g * P, (g + 1) * P)
+                        nc.tensor.matmul_mx(
+                            out=planes[b][:, (2 + i) * P : (3 + i) * P],
+                            lhsT=r_codes[:, units].bitcast(FP8X4),
+                            lhsT_scale=r_scales[:, units],
+                            rhs=sup_codes[s, i][:, nodes].bitcast(FP8X4),
+                            rhs_scale=sup_scales[s, i][:, nodes],
+                            start=(g == 0),
+                            stop=(g == PASSES - 1),
+                        )
+            for b in range(BATCH):
+                copy = nc.scalar.copy if b == 0 else nc.vector.tensor_copy
+                first = (b * ROWS + j) * P * PACK
+                copy(
+                    out=hc_grouped[q][:, first : first + P * PACK].rearrange("p (m t) -> p m t", t=PACK),
+                    in_=planes[b][:].rearrange("p (t m) -> p m t", t=PACK),
+                )
+
+        def finish_round(q):
+            rows = slice(q * ROUND, (q + 1) * ROUND)
+            hc_codes = ending.tile([P, BANK], U32, align_bytes=64)
+            hc_scales = ending.tile([P, BANK], U8, align_bytes=64)
+            nc.vector.quantize_mx(out=hc_codes[:].bitcast(FP8X4), scales=hc_scales[:], in_=hc_grouped[q][:])
+            pre = single.tile([P, BANK], F32)
+            for tile_index in range(BATCH * ROWS):
+                nodes = slice(tile_index * P, (tile_index + 1) * P)
+                nc.tensor.matmul_mx(
+                    out=pre[:, nodes],
+                    lhsT=hc_codes[:, nodes].bitcast(FP8X4),
+                    lhsT_scale=hc_scales[:, nodes],
+                    rhs=ck_codes[:].bitcast(FP8X4),
+                    rhs_scale=ck_scales[:],
+                    start=True,
+                    stop=True,
+                )
+            cand = ending.tile([P, BANK], F32)
+            nc.scalar.activation(out=cand[:], in_=pre[:], func=TANH)
+            diff = ending.tile([P, BANK], F32)
+            nc.vector.tensor_tensor(
+                out=diff[:].rearrange("p (b j k) -> p b j k", b=BATCH, j=ROWS),
+                in0=prev_bank[q][:].bitcast(BF16).rearrange("p (b k j) -> p b j k", b=BATCH, j=ROWS),
+                in1=cand[:].rearrange("p (b j k) -> p b j k", b=BATCH, j=ROWS),
+                op=ALU.subtract,
+            )
+            nc.vector.tensor_tensor(out=diff[:], in0=diff[:], in1=u_raw[q][:], op=ALU.mult)
+            z = ending.tile([P, BANK], F32)
+            nc.vector.tensor_tensor(out=z[:], in0=diff[:], in1=cand[:], op=ALU.add)
+            nc.gpsimd.dma_start(
+                out=out_rows[:, rows, :].rearrange("b (p j) k -> p b (j k)", j=ROWS),
+                in_=z[:].rearrange("p (b x) -> p b x", b=BATCH),
+            )
+
+        quantise_supports(0)
+        for s in range(STEPS):
+            q, j = divmod(s, ROWS)
+            if j == ROWS - 1:
+                transpose_state(q)
+            if s + 1 < STEPS:
+                quantise_supports(s + 1)
+            diffuse(s)
+            if j == 0 and q > 0:
+                finish_round(q - 1)
+            if j == 0 and q + AHEAD < ROUNDS:
+                load_round(q + AHEAD)
+        finish_round(ROUNDS - 1)

@@ -50,12 +50,13 @@ def tile_gcrnncell_pb_kernel(tc, r_prev, h_diff, u, state, support0, support1, c
     with ExitStack() as stack:
         keep = stack.enter_context(tc.tile_pool(name="keep", bufs=1))
         big_in = stack.enter_context(tc.tile_pool(name="big_in", bufs=AHEAD))
-        small_in = stack.enter_context(tc.tile_pool(name="small_in", bufs=AHEAD + 1))
+        small_in = stack.enter_context(tc.tile_pool(name="small_in", bufs=AHEAD + 2))
         moving = stack.enter_context(tc.tile_pool(name="moving", bufs=4))
         ending = stack.enter_context(tc.tile_pool(name="ending", bufs=2))
-        banks = stack.enter_context(tc.psum_pool(name="banks", bufs=3))
-        sums = stack.enter_context(tc.psum_pool(name="sums", bufs=3))
+        banks = stack.enter_context(tc.psum_pool(name="banks", bufs=4))
+        sums = stack.enter_context(tc.psum_pool(name="sums", bufs=BATCH))
         single = stack.enter_context(tc.psum_pool(name="single", bufs=1))
+        stack.enter_context(tc.manual_schedule())
 
         sup_raw = {}
         h_raw = {}
@@ -126,8 +127,12 @@ def tile_gcrnncell_pb_kernel(tc, r_prev, h_diff, u, state, support0, support1, c
 
         sup_codes = {}
         sup_scales = {}
+        planes = {}
         hc_grouped = {}
+        hc_codes = {}
+        hc_scales = {}
         prev_bank = {}
+        cand = {}
 
         def quantise_supports(s):
             q, j = divmod(s, ROWS)
@@ -158,15 +163,12 @@ def tile_gcrnncell_pb_kernel(tc, r_prev, h_diff, u, state, support0, support1, c
 
         def diffuse(s):
             q, j = divmod(s, ROWS)
-            if j == 0:
-                hc_grouped[q] = ending.tile([P, BATCH * ROWS * P * PACK], BF16, name="hc", tag="hc", align_bytes=64)
-            planes = []
             for b in range(BATCH):
-                planes.append(sums.tile([P, BANK], F32, name="planes", tag="planes"))
+                planes[s, b] = sums.tile([P, BANK], F32, name="planes", tag="planes")
                 for t in range(FEATS // P):
                     first = (b * ROWS + j) * FEATS + t * P
                     nc.tensor.matmul(
-                        out=planes[b][:, t * P : (t + 1) * P],
+                        out=planes[s, b][:, t * P : (t + 1) * P],
                         lhsT=h_raw[q][:, first : first + P],
                         rhs=ident_bf16[:],
                         start=True,
@@ -178,7 +180,7 @@ def tile_gcrnncell_pb_kernel(tc, r_prev, h_diff, u, state, support0, support1, c
                         units = slice((b * PASSES + g) * UNITS, (b * PASSES + g + 1) * UNITS)
                         nodes = slice(g * P, (g + 1) * P)
                         nc.tensor.matmul_mx(
-                            out=planes[b][:, (2 + i) * P : (3 + i) * P],
+                            out=planes[s, b][:, (2 + i) * P : (3 + i) * P],
                             lhsT=r_codes[:, units].bitcast(FP8X4),
                             lhsT_scale=r_scales[:, units],
                             rhs=sup_codes[s, i][:, nodes].bitcast(FP8X4),
@@ -186,43 +188,52 @@ def tile_gcrnncell_pb_kernel(tc, r_prev, h_diff, u, state, support0, support1, c
                             start=(g == 0),
                             stop=(g == PASSES - 1),
                         )
+
+        def collect(s):
+            q, j = divmod(s, ROWS)
+            if j == 0:
+                hc_grouped[q] = ending.tile([P, BATCH * ROWS * P * PACK], BF16, name="hc", tag="hc", align_bytes=64)
             for b in range(BATCH):
                 copy = nc.scalar.copy if b == 0 else nc.vector.tensor_copy
                 first = (b * ROWS + j) * P * PACK
                 copy(
                     out=hc_grouped[q][:, first : first + P * PACK].rearrange("p (m t) -> p m t", t=PACK),
-                    in_=planes[b][:].rearrange("p (t m) -> p m t", t=PACK),
+                    in_=planes[s, b][:].rearrange("p (t m) -> p m t", t=PACK),
                 )
 
-        def finish_round(q):
-            rows = slice(q * ROUND, (q + 1) * ROUND)
-            hc_codes = ending.tile([P, BANK], U32, align_bytes=64)
-            hc_scales = ending.tile([P, BANK], U8, align_bytes=64)
-            nc.vector.quantize_mx(out=hc_codes[:].bitcast(FP8X4), scales=hc_scales[:], in_=hc_grouped[q][:])
+        def quantise_hc(q):
+            hc_codes[q] = ending.tile([P, BANK], U32, name="hc_codes", tag="hc_codes", align_bytes=64)
+            hc_scales[q] = ending.tile([P, BANK], U8, name="hc_scales", tag="hc_scales", align_bytes=64)
+            nc.vector.quantize_mx(out=hc_codes[q][:].bitcast(FP8X4), scales=hc_scales[q][:], in_=hc_grouped[q][:])
+
+        def candidate(q):
             pre = single.tile([P, BANK], F32)
             for tile_index in range(BATCH * ROWS):
                 nodes = slice(tile_index * P, (tile_index + 1) * P)
                 nc.tensor.matmul_mx(
                     out=pre[:, nodes],
-                    lhsT=hc_codes[:, nodes].bitcast(FP8X4),
-                    lhsT_scale=hc_scales[:, nodes],
+                    lhsT=hc_codes[q][:, nodes].bitcast(FP8X4),
+                    lhsT_scale=hc_scales[q][:, nodes],
                     rhs=ck_codes[:].bitcast(FP8X4),
                     rhs_scale=ck_scales[:],
                     start=True,
                     stop=True,
                 )
-            cand = ending.tile([P, BANK], F32)
-            nc.scalar.activation(out=cand[:], in_=pre[:], func=TANH)
+            cand[q] = ending.tile([P, BANK], F32, name="cand", tag="cand")
+            nc.scalar.activation(out=cand[q][:], in_=pre[:], func=TANH)
+
+        def blend(q):
+            rows = slice(q * ROUND, (q + 1) * ROUND)
             diff = ending.tile([P, BANK], F32)
             nc.vector.tensor_tensor(
                 out=diff[:].rearrange("p (b j k) -> p b j k", b=BATCH, j=ROWS),
                 in0=prev_bank[q][:].bitcast(BF16).rearrange("p (b k j) -> p b j k", b=BATCH, j=ROWS),
-                in1=cand[:].rearrange("p (b j k) -> p b j k", b=BATCH, j=ROWS),
+                in1=cand[q][:].rearrange("p (b j k) -> p b j k", b=BATCH, j=ROWS),
                 op=ALU.subtract,
             )
             nc.vector.tensor_tensor(out=diff[:], in0=diff[:], in1=u_raw[q][:], op=ALU.mult)
             z = ending.tile([P, BANK], F32)
-            nc.vector.tensor_tensor(out=z[:], in0=diff[:], in1=cand[:], op=ALU.add)
+            nc.vector.tensor_tensor(out=z[:], in0=diff[:], in1=cand[q][:], op=ALU.add)
             nc.gpsimd.dma_start(
                 out=out_rows[:, rows, :].rearrange("b (p j) k -> p b (j k)", j=ROWS),
                 in_=z[:].rearrange("p (b x) -> p b x", b=BATCH),
@@ -231,13 +242,22 @@ def tile_gcrnncell_pb_kernel(tc, r_prev, h_diff, u, state, support0, support1, c
         quantise_supports(0)
         for s in range(STEPS):
             q, j = divmod(s, ROWS)
-            if j == ROWS - 1:
-                transpose_state(q)
+            if s > 0:
+                collect(s - 1)
+            if j == 0 and q > 0:
+                quantise_hc(q - 1)
+                transpose_state(q - 1)
+            if j == 1 and q > 0:
+                blend(q - 1)
             if s + 1 < STEPS:
                 quantise_supports(s + 1)
-            diffuse(s)
             if j == 0 and q > 0:
-                finish_round(q - 1)
+                candidate(q - 1)
+            diffuse(s)
             if j == 0 and q + AHEAD < ROUNDS:
                 load_round(q + AHEAD)
-        finish_round(ROUNDS - 1)
+        collect(STEPS - 1)
+        quantise_hc(ROUNDS - 1)
+        transpose_state(ROUNDS - 1)
+        candidate(ROUNDS - 1)
+        blend(ROUNDS - 1)

@@ -25,6 +25,10 @@ ROWS = 2
 ROUND = P * ROWS
 ROUNDS = NODES // ROUND
 STEPS = ROUNDS * ROWS
+HALVES = 2
+HALF_STEPS = STEPS * HALVES
+PER_ROUND = ROWS * HALVES
+LEAD = 2
 AHEAD = 3
 
 FLOPS = 2 * SUPPORTS * BATCH * UNITS * NODES * NODES + 2 * BATCH * NODES * (FEATS + SUPPORTS * UNITS) * UNITS
@@ -36,7 +40,7 @@ def transpose_512_words(nc, banks, identity, copy, words_in, words_out):
         cols = slice(block * P, (block + 1) * P)
         nc.tensor.transpose(out=bank[:, cols], in_=words_in[:, cols], identity=identity)
     copy(
-        out=words_out.rearrange("p (g r u) -> p g r u", g=2, u=2),
+        out=words_out.rearrange("p g (r u) -> p g r u", u=2),
         in_=bank[:].rearrange("p (g u r) -> p g r u", g=2, u=2),
     )
 
@@ -51,7 +55,7 @@ def tile_gcrnncell_pb_kernel(tc, r_prev, h_diff, u, state, support0, support1, c
         keep = stack.enter_context(tc.tile_pool(name="keep", bufs=1))
         big_in = stack.enter_context(tc.tile_pool(name="big_in", bufs=AHEAD))
         small_in = stack.enter_context(tc.tile_pool(name="small_in", bufs=AHEAD + 2))
-        moving = stack.enter_context(tc.tile_pool(name="moving", bufs=4))
+        moving = stack.enter_context(tc.tile_pool(name="moving", bufs=LEAD + 2))
         ending = stack.enter_context(tc.tile_pool(name="ending", bufs=2))
         banks = stack.enter_context(tc.psum_pool(name="banks", bufs=4))
         sums = stack.enter_context(tc.psum_pool(name="sums", bufs=BATCH))
@@ -112,7 +116,7 @@ def tile_gcrnncell_pb_kernel(tc, r_prev, h_diff, u, state, support0, support1, c
                 ident_f32[:],
                 nc.scalar.copy if piece % 2 == 0 else nc.vector.tensor_copy,
                 r_raw[:].bitcast(F32)[:, words],
-                r_grouped[:].bitcast(F32)[:, words],
+                r_grouped[:].bitcast(F32)[:, words].rearrange("p (g x) -> p g x", g=2),
             )
         nc.vector.quantize_mx(out=r_codes[:].bitcast(FP8X4), scales=r_scales[:], in_=r_grouped[:])
 
@@ -133,35 +137,27 @@ def tile_gcrnncell_pb_kernel(tc, r_prev, h_diff, u, state, support0, support1, c
         hc_scales = {}
         prev_bank = {}
         cand = {}
+        diff = {}
 
-        def quantise_supports(s):
+        def quantise_supports(h):
+            s, half = divmod(h, HALVES)
             q, j = divmod(s, ROWS)
+            grouped = moving.tile([P, PACK * BANK], BF16, align_bytes=64)
             for i in range(SUPPORTS):
-                grouped = moving.tile([P, PACK * BANK], BF16, align_bytes=64)
-                for half in range(2):
-                    transpose_512_words(
-                        nc,
-                        banks,
-                        ident_f32[:],
-                        nc.scalar.copy,
-                        sup_raw[q, i][:].bitcast(F32)[:, (2 * j + half) * BANK : (2 * j + half + 1) * BANK],
-                        grouped[:].bitcast(F32)[:, half * BANK : (half + 1) * BANK],
-                    )
-                sup_codes[s, i] = moving.tile([P, BANK], U32, name="codes", tag="codes", align_bytes=64)
-                sup_scales[s, i] = moving.tile([P, BANK], U8, name="scales", tag="scales", align_bytes=64)
-                nc.vector.quantize_mx(
-                    out=sup_codes[s, i][:].bitcast(FP8X4), scales=sup_scales[s, i][:], in_=grouped[:]
+                first = (j * HALVES + half) * BANK
+                transpose_512_words(
+                    nc,
+                    banks,
+                    ident_f32[:],
+                    nc.scalar.copy,
+                    sup_raw[q, i][:].bitcast(F32)[:, first : first + BANK],
+                    grouped[:].bitcast(F32).rearrange("p (g i x) -> p g i x", g=2, i=SUPPORTS)[:, :, i, :],
                 )
+            sup_codes[h] = moving.tile([P, BANK], U32, name="codes", tag="codes", align_bytes=64)
+            sup_scales[h] = moving.tile([P, BANK], U8, name="scales", tag="scales", align_bytes=64)
+            nc.vector.quantize_mx(out=sup_codes[h][:].bitcast(FP8X4), scales=sup_scales[h][:], in_=grouped[:])
 
-        def transpose_state(q):
-            prev_bank[q] = single.tile([P, BATCH * UNITS], F32, name="prev", tag="prev")
-            for b in range(BATCH):
-                cols = slice(b * P, (b + 1) * P)
-                nc.tensor.transpose(
-                    out=prev_bank[q][:, cols], in_=state_raw[q][:].bitcast(F32)[:, cols], identity=ident_f32[:]
-                )
-
-        def diffuse(s):
+        def features(s):
             q, j = divmod(s, ROWS)
             for b in range(BATCH):
                 planes[s, b] = sums.tile([P, BANK], F32, name="planes", tag="planes")
@@ -174,20 +170,23 @@ def tile_gcrnncell_pb_kernel(tc, r_prev, h_diff, u, state, support0, support1, c
                         start=True,
                         stop=True,
                     )
-            for i in range(SUPPORTS):
-                for b in range(BATCH):
-                    for g in range(PASSES):
-                        units = slice((b * PASSES + g) * UNITS, (b * PASSES + g + 1) * UNITS)
-                        nodes = slice(g * P, (g + 1) * P)
-                        nc.tensor.matmul_mx(
-                            out=planes[s, b][:, (2 + i) * P : (3 + i) * P],
-                            lhsT=r_codes[:, units].bitcast(FP8X4),
-                            lhsT_scale=r_scales[:, units],
-                            rhs=sup_codes[s, i][:, nodes].bitcast(FP8X4),
-                            rhs_scale=sup_scales[s, i][:, nodes],
-                            start=(g == 0),
-                            stop=(g == PASSES - 1),
-                        )
+
+        def diffuse(h):
+            s, half = divmod(h, HALVES)
+            for b in range(BATCH):
+                for local in range(PASSES // HALVES):
+                    g = half * (PASSES // HALVES) + local
+                    units = slice((b * PASSES + g) * UNITS, (b * PASSES + g + 1) * UNITS)
+                    nodes = slice(local * SUPPORTS * P, (local + 1) * SUPPORTS * P)
+                    nc.tensor.matmul_mx(
+                        out=planes[s, b][:, FEATS:BANK],
+                        lhsT=r_codes[:, units].bitcast(FP8X4),
+                        lhsT_scale=r_scales[:, units],
+                        rhs=sup_codes[h][:, nodes].bitcast(FP8X4),
+                        rhs_scale=sup_scales[h][:, nodes],
+                        start=(g == 0),
+                        stop=(g == PASSES - 1),
+                    )
 
         def collect(s):
             q, j = divmod(s, ROWS)
@@ -206,6 +205,14 @@ def tile_gcrnncell_pb_kernel(tc, r_prev, h_diff, u, state, support0, support1, c
             hc_scales[q] = ending.tile([P, BANK], U8, name="hc_scales", tag="hc_scales", align_bytes=64)
             nc.vector.quantize_mx(out=hc_codes[q][:].bitcast(FP8X4), scales=hc_scales[q][:], in_=hc_grouped[q][:])
 
+        def transpose_state(q):
+            prev_bank[q] = single.tile([P, BATCH * UNITS], F32, name="prev", tag="prev")
+            for b in range(BATCH):
+                cols = slice(b * P, (b + 1) * P)
+                nc.tensor.transpose(
+                    out=prev_bank[q][:, cols], in_=state_raw[q][:].bitcast(F32)[:, cols], identity=ident_f32[:]
+                )
+
         def candidate(q):
             pre = single.tile([P, BANK], F32)
             for tile_index in range(BATCH * ROWS):
@@ -222,42 +229,52 @@ def tile_gcrnncell_pb_kernel(tc, r_prev, h_diff, u, state, support0, support1, c
             cand[q] = ending.tile([P, BANK], F32, name="cand", tag="cand")
             nc.scalar.activation(out=cand[q][:], in_=pre[:], func=TANH)
 
-        def blend(q):
-            rows = slice(q * ROUND, (q + 1) * ROUND)
-            diff = ending.tile([P, BANK], F32)
+        def blend_first(q):
+            diff[q] = ending.tile([P, BANK], F32, name="diff", tag="diff")
             nc.vector.tensor_tensor(
-                out=diff[:].rearrange("p (b j k) -> p b j k", b=BATCH, j=ROWS),
+                out=diff[q][:].rearrange("p (b j k) -> p b j k", b=BATCH, j=ROWS),
                 in0=prev_bank[q][:].bitcast(BF16).rearrange("p (b k j) -> p b j k", b=BATCH, j=ROWS),
                 in1=cand[q][:].rearrange("p (b j k) -> p b j k", b=BATCH, j=ROWS),
                 op=ALU.subtract,
             )
-            nc.vector.tensor_tensor(out=diff[:], in0=diff[:], in1=u_raw[q][:], op=ALU.mult)
+
+        def blend_last(q):
+            rows = slice(q * ROUND, (q + 1) * ROUND)
+            nc.vector.tensor_tensor(out=diff[q][:], in0=diff[q][:], in1=u_raw[q][:], op=ALU.mult)
             z = ending.tile([P, BANK], F32)
-            nc.vector.tensor_tensor(out=z[:], in0=diff[:], in1=cand[q][:], op=ALU.add)
+            nc.vector.tensor_tensor(out=z[:], in0=diff[q][:], in1=cand[q][:], op=ALU.add)
             nc.gpsimd.dma_start(
                 out=out_rows[:, rows, :].rearrange("b (p j) k -> p b (j k)", j=ROWS),
                 in_=z[:].rearrange("p (b x) -> p b x", b=BATCH),
             )
 
-        quantise_supports(0)
-        for s in range(STEPS):
-            q, j = divmod(s, ROWS)
-            if s > 0:
+        for h in range(LEAD):
+            quantise_supports(h)
+        for h in range(HALF_STEPS):
+            q, stage = divmod(h, PER_ROUND)
+            s, half = divmod(h, HALVES)
+            if half == 0 and s > 0:
                 collect(s - 1)
-            if j == 0 and q > 0:
+            if q > 0 and stage == 0:
                 quantise_hc(q - 1)
+            if q > 0 and stage == 1:
                 transpose_state(q - 1)
-            if j == 1 and q > 0:
-                blend(q - 1)
-            if s + 1 < STEPS:
-                quantise_supports(s + 1)
-            if j == 0 and q > 0:
+            if q > 0 and stage == 2:
+                blend_first(q - 1)
+            if q > 0 and stage == 3:
+                blend_last(q - 1)
+            if h + LEAD < HALF_STEPS:
+                quantise_supports(h + LEAD)
+            if half == 0:
+                features(s)
+            if q > 0 and stage == 1:
                 candidate(q - 1)
-            diffuse(s)
-            if j == 0 and q + AHEAD < ROUNDS:
+            diffuse(h)
+            if stage == PER_ROUND - 1 - LEAD and q + AHEAD < ROUNDS:
                 load_round(q + AHEAD)
         collect(STEPS - 1)
         quantise_hc(ROUNDS - 1)
         transpose_state(ROUNDS - 1)
         candidate(ROUNDS - 1)
-        blend(ROUNDS - 1)
+        blend_first(ROUNDS - 1)
+        blend_last(ROUNDS - 1)

@@ -21,15 +21,13 @@ PACK = 4
 K_PASS = P * PACK
 PASSES = NODES // K_PASS
 BANK = 512
+PAIR = 2
 ROWS = 2
 ROUND = P * ROWS
 ROUNDS = NODES // ROUND
 STEPS = ROUNDS * ROWS
-HALVES = 2
-HALF_STEPS = STEPS * HALVES
-PER_ROUND = ROWS * HALVES
-LEAD = 2
 AHEAD = 3
+FIRST_PIECES = 4
 
 FLOPS = 2 * SUPPORTS * BATCH * UNITS * NODES * NODES + 2 * BATCH * NODES * (FEATS + SUPPORTS * UNITS) * UNITS
 
@@ -41,7 +39,7 @@ def transpose_512_words(nc, banks, identity, copy, words_in, words_out):
         nc.tensor.transpose(out=bank[:, cols], in_=words_in[:, cols], identity=identity)
     copy(
         out=words_out.rearrange("p g (r u) -> p g r u", u=2),
-        in_=bank[:].rearrange("p (g u r) -> p g r u", g=2, u=2),
+        in_=bank[:].rearrange("p (g u r) -> p g r u", g=PAIR, u=2),
     )
 
 
@@ -55,8 +53,8 @@ def tile_gcrnncell_pb_kernel(tc, r_prev, h_diff, u, state, support0, support1, c
         keep = stack.enter_context(tc.tile_pool(name="keep", bufs=1))
         big_in = stack.enter_context(tc.tile_pool(name="big_in", bufs=AHEAD))
         small_in = stack.enter_context(tc.tile_pool(name="small_in", bufs=AHEAD + 2))
-        moving = stack.enter_context(tc.tile_pool(name="moving", bufs=LEAD + 2))
-        ending = stack.enter_context(tc.tile_pool(name="ending", bufs=2))
+        moving = stack.enter_context(tc.tile_pool(name="moving", bufs=6))
+        ending = stack.enter_context(tc.tile_pool(name="ending", bufs=3))
         banks = stack.enter_context(tc.psum_pool(name="banks", bufs=4))
         sums = stack.enter_context(tc.psum_pool(name="sums", bufs=BATCH))
         single = stack.enter_context(tc.psum_pool(name="single", bufs=1))
@@ -67,95 +65,101 @@ def tile_gcrnncell_pb_kernel(tc, r_prev, h_diff, u, state, support0, support1, c
         u_raw = {}
         state_raw = {}
 
-        def load_round(q):
-            rows = slice(q * ROUND, (q + 1) * ROUND)
-            for i in range(SUPPORTS):
-                sup_raw[q, i] = big_in.tile([P, ROWS * NODES], BF16, name="sup", tag="sup%d" % i)
+        def fetch(q):
+            if q < ROUNDS:
+                rows = slice(q * ROUND, (q + 1) * ROUND)
+                for i in range(SUPPORTS):
+                    sup_raw[q, i] = big_in.tile([P, ROWS * NODES], BF16, name="sup", tag="sup%d" % i)
+                pieces = max(1, FIRST_PIECES >> q)
+                width = ROWS * NODES // pieces
+                for piece in range(pieces):
+                    cols = slice(piece * width, (piece + 1) * width)
+                    for i in range(SUPPORTS):
+                        nc.sync.dma_start(
+                            out=sup_raw[q, i][:, cols],
+                            in_=supports[i][rows, :].rearrange("(p j) n -> p (j n)", j=ROWS)[:, cols],
+                        )
+                h_raw[q] = small_in.tile([P, BATCH * ROWS * FEATS], BF16, name="h", tag="h")
                 nc.sync.dma_start(
-                    out=sup_raw[q, i][:], in_=supports[i][rows, :].rearrange("(p j) n -> p (j n)", j=ROWS)
+                    out=h_raw[q][:].rearrange("p (b x) -> p b x", b=BATCH),
+                    in_=h_diff[:, rows, :].rearrange("b (p j) c -> p b (j c)", j=ROWS),
                 )
-            h_raw[q] = small_in.tile([P, BATCH * ROWS * FEATS], BF16, name="h", tag="h")
-            nc.sync.dma_start(
-                out=h_raw[q][:].rearrange("p (b x) -> p b x", b=BATCH),
-                in_=h_diff[:, rows, :].rearrange("b (p j) c -> p b (j c)", j=ROWS),
-            )
-            state_raw[q] = small_in.tile([P, BATCH * ROUND], BF16, name="st", tag="st")
-            nc.sync.dma_start(
-                out=state_raw[q][:].rearrange("p (b n) -> p b n", b=BATCH), in_=state_rows[:, :, rows]
-            )
-            u_raw[q] = small_in.tile([P, BATCH * ROWS * UNITS], BF16, name="gate", tag="gate")
-            nc.sync.dma_start(
-                out=u_raw[q][:].rearrange("p (b x) -> p b x", b=BATCH),
-                in_=u[:, rows, :].rearrange("b (p j) k -> p b (j k)", j=ROWS),
-            )
+            if q >= 1:
+                rows = slice((q - 1) * ROUND, q * ROUND)
+                state_raw[q - 1] = small_in.tile([P, BATCH * ROUND], BF16, name="st", tag="st")
+                nc.sync.dma_start(
+                    out=state_raw[q - 1][:].rearrange("p (b n) -> p b n", b=BATCH), in_=state_rows[:, :, rows]
+                )
+                u_raw[q - 1] = small_in.tile([P, BATCH * ROWS * UNITS], BF16, name="gate", tag="gate")
+                nc.sync.dma_start(
+                    out=u_raw[q - 1][:].rearrange("p (b x) -> p b x", b=BATCH),
+                    in_=u[:, rows, :].rearrange("b (p j) k -> p b (j k)", j=ROWS),
+                )
 
         r_raw = keep.tile([P, BATCH * NODES], BF16)
-        nc.sync.dma_start(
-            out=r_raw[:].rearrange("p (b n) -> p b n", b=BATCH), in_=r_prev.rearrange("b k n -> k b n")
-        )
+        for b in range(BATCH):
+            for pair in range(PASSES // PAIR):
+                cols = slice(pair * PAIR * K_PASS, (pair + 1) * PAIR * K_PASS)
+                first = b * NODES + pair * PAIR * K_PASS
+                nc.sync.dma_start(out=r_raw[:, first : first + PAIR * K_PASS], in_=r_prev[b, :, cols])
+        fetch(0)
         ck_raw = keep.tile([P, PACK * UNITS], BF16)
         nc.sync.dma_start(
             out=ck_raw[:].rearrange("p (t k) -> p t k", t=PACK), in_=c_kernel.rearrange("(t p) k -> p t k", p=P)
         )
-        for q in range(AHEAD):
-            load_round(q)
+        for q in range(1, AHEAD):
+            fetch(q)
 
         ident_f32 = keep.tile([P, P], F32)
         make_identity(nc, ident_f32[:])
         ident_bf16 = keep.tile([P, P], BF16)
         make_identity(nc, ident_bf16[:])
 
+        both_engines = (nc.scalar.copy, nc.vector.tensor_copy)
+        scalar_only = (nc.scalar.copy, nc.scalar.copy)
+
         r_grouped = keep.tile([P, BATCH * NODES], BF16, align_bytes=64)
         r_codes = keep.tile([P, BATCH * PASSES * UNITS], U32, align_bytes=64)
         r_scales = keep.tile([P, BATCH * PASSES * UNITS], U8, align_bytes=64)
-        for piece in range(BATCH * NODES // (2 * BANK)):
+        for piece in range(BATCH * PASSES // PAIR):
             words = slice(piece * BANK, (piece + 1) * BANK)
             transpose_512_words(
                 nc,
                 banks,
                 ident_f32[:],
-                nc.scalar.copy if piece % 2 == 0 else nc.vector.tensor_copy,
+                both_engines[piece % 2],
                 r_raw[:].bitcast(F32)[:, words],
-                r_grouped[:].bitcast(F32)[:, words].rearrange("p (g x) -> p g x", g=2),
+                r_grouped[:].bitcast(F32)[:, words].rearrange("p (g x) -> p g x", g=PAIR),
             )
         nc.vector.quantize_mx(out=r_codes[:].bitcast(FP8X4), scales=r_scales[:], in_=r_grouped[:])
-
-        ck_grouped = keep.tile([P, UNITS * PACK], BF16, align_bytes=64)
-        ck_codes = keep.tile([P, UNITS], U32, align_bytes=64)
-        ck_scales = keep.tile([P, UNITS], U8, align_bytes=64)
-        nc.vector.tensor_copy(
-            out=ck_grouped[:].rearrange("p (k t) -> p k t", t=PACK),
-            in_=ck_raw[:].rearrange("p (t k) -> p k t", t=PACK),
-        )
-        nc.vector.quantize_mx(out=ck_codes[:].bitcast(FP8X4), scales=ck_scales[:], in_=ck_grouped[:])
 
         sup_codes = {}
         sup_scales = {}
         planes = {}
-        hc_grouped = {}
         hc_codes = {}
         hc_scales = {}
-        prev_bank = {}
+        kept = {}
         cand = {}
-        diff = {}
 
-        def quantise_supports(h):
-            s, half = divmod(h, HALVES)
+        def quantise_supports(s, copies):
             q, j = divmod(s, ROWS)
-            grouped = moving.tile([P, PACK * BANK], BF16, align_bytes=64)
-            for i in range(SUPPORTS):
-                first = (j * HALVES + half) * BANK
-                transpose_512_words(
-                    nc,
-                    banks,
-                    ident_f32[:],
-                    nc.scalar.copy,
-                    sup_raw[q, i][:].bitcast(F32)[:, first : first + BANK],
-                    grouped[:].bitcast(F32).rearrange("p (g i x) -> p g i x", g=2, i=SUPPORTS)[:, :, i, :],
+            for pair in range(PASSES // PAIR):
+                grouped = moving.tile([P, PACK * BANK], BF16, align_bytes=64)
+                for i in range(SUPPORTS):
+                    first = (j * PASSES // PAIR + pair) * BANK
+                    transpose_512_words(
+                        nc,
+                        banks,
+                        ident_f32[:],
+                        copies[i],
+                        sup_raw[q, i][:].bitcast(F32)[:, first : first + BANK],
+                        grouped[:].bitcast(F32).rearrange("p (g i x) -> p g i x", g=PAIR, i=SUPPORTS)[:, :, i, :],
+                    )
+                sup_codes[s, pair] = moving.tile([P, BANK], U32, name="codes", tag="codes", align_bytes=64)
+                sup_scales[s, pair] = moving.tile([P, BANK], U8, name="scales", tag="scales", align_bytes=64)
+                nc.vector.quantize_mx(
+                    out=sup_codes[s, pair][:].bitcast(FP8X4), scales=sup_scales[s, pair][:], in_=grouped[:]
                 )
-            sup_codes[h] = moving.tile([P, BANK], U32, name="codes", tag="codes", align_bytes=64)
-            sup_scales[h] = moving.tile([P, BANK], U8, name="scales", tag="scales", align_bytes=64)
-            nc.vector.quantize_mx(out=sup_codes[h][:].bitcast(FP8X4), scales=sup_scales[h][:], in_=grouped[:])
 
         def features(s):
             q, j = divmod(s, ROWS)
@@ -171,110 +175,114 @@ def tile_gcrnncell_pb_kernel(tc, r_prev, h_diff, u, state, support0, support1, c
                         stop=True,
                     )
 
-        def diffuse(h):
-            s, half = divmod(h, HALVES)
-            for b in range(BATCH):
-                for local in range(PASSES // HALVES):
-                    g = half * (PASSES // HALVES) + local
+        def diffuse(s):
+            for g in range(PASSES):
+                pair, local = divmod(g, PAIR)
+                nodes = slice(local * SUPPORTS * P, (local + 1) * SUPPORTS * P)
+                for b in range(BATCH):
                     units = slice((b * PASSES + g) * UNITS, (b * PASSES + g + 1) * UNITS)
-                    nodes = slice(local * SUPPORTS * P, (local + 1) * SUPPORTS * P)
                     nc.tensor.matmul_mx(
                         out=planes[s, b][:, FEATS:BANK],
                         lhsT=r_codes[:, units].bitcast(FP8X4),
                         lhsT_scale=r_scales[:, units],
-                        rhs=sup_codes[h][:, nodes].bitcast(FP8X4),
-                        rhs_scale=sup_scales[h][:, nodes],
+                        rhs=sup_codes[s, pair][:, nodes].bitcast(FP8X4),
+                        rhs_scale=sup_scales[s, pair][:, nodes],
                         start=(g == 0),
                         stop=(g == PASSES - 1),
                     )
 
         def collect(s):
-            q, j = divmod(s, ROWS)
-            if j == 0:
-                hc_grouped[q] = ending.tile([P, BATCH * ROWS * P * PACK], BF16, name="hc", tag="hc", align_bytes=64)
+            hc_grouped = ending.tile([P, BATCH * P * PACK], BF16, align_bytes=64)
             for b in range(BATCH):
-                copy = nc.scalar.copy if b == 0 else nc.vector.tensor_copy
-                first = (b * ROWS + j) * P * PACK
-                copy(
-                    out=hc_grouped[q][:, first : first + P * PACK].rearrange("p (m t) -> p m t", t=PACK),
+                both_engines[b](
+                    out=hc_grouped[:, b * P * PACK : (b + 1) * P * PACK].rearrange("p (m t) -> p m t", t=PACK),
                     in_=planes[s, b][:].rearrange("p (t m) -> p m t", t=PACK),
                 )
+            hc_codes[s] = ending.tile([P, BATCH * P], U32, name="hc_codes", tag="hc_codes", align_bytes=64)
+            hc_scales[s] = ending.tile([P, BATCH * P], U8, name="hc_scales", tag="hc_scales", align_bytes=64)
+            nc.vector.quantize_mx(out=hc_codes[s][:].bitcast(FP8X4), scales=hc_scales[s][:], in_=hc_grouped[:])
 
-        def quantise_hc(q):
-            hc_codes[q] = ending.tile([P, BANK], U32, name="hc_codes", tag="hc_codes", align_bytes=64)
-            hc_scales[q] = ending.tile([P, BANK], U8, name="hc_scales", tag="hc_scales", align_bytes=64)
-            nc.vector.quantize_mx(out=hc_codes[q][:].bitcast(FP8X4), scales=hc_scales[q][:], in_=hc_grouped[q][:])
-
-        def transpose_state(q):
-            prev_bank[q] = single.tile([P, BATCH * UNITS], F32, name="prev", tag="prev")
+        def old_part(q):
+            prev_bank = single.tile([P, BATCH * UNITS], F32)
             for b in range(BATCH):
                 cols = slice(b * P, (b + 1) * P)
                 nc.tensor.transpose(
-                    out=prev_bank[q][:, cols], in_=state_raw[q][:].bitcast(F32)[:, cols], identity=ident_f32[:]
+                    out=prev_bank[:, cols], in_=state_raw[q][:].bitcast(F32)[:, cols], identity=ident_f32[:]
                 )
+            kept[q] = ending.tile([P, BANK], F32, name="kept", tag="kept")
+            nc.vector.tensor_tensor(
+                out=kept[q][:].rearrange("p (b j k) -> p b j k", b=BATCH, j=ROWS),
+                in0=prev_bank[:].bitcast(BF16).rearrange("p (b k j) -> p b j k", b=BATCH, j=ROWS),
+                in1=u_raw[q][:].rearrange("p (b j k) -> p b j k", b=BATCH, j=ROWS),
+                op=ALU.mult,
+            )
 
-        def candidate(q):
-            pre = single.tile([P, BANK], F32)
-            for tile_index in range(BATCH * ROWS):
-                nodes = slice(tile_index * P, (tile_index + 1) * P)
+        def candidate(s):
+            pre = single.tile([P, BATCH * UNITS], F32)
+            for b in range(BATCH):
+                nodes = slice(b * P, (b + 1) * P)
                 nc.tensor.matmul_mx(
-                    out=pre[:, nodes],
-                    lhsT=hc_codes[q][:, nodes].bitcast(FP8X4),
-                    lhsT_scale=hc_scales[q][:, nodes],
+                    out=pre[:, b * UNITS : (b + 1) * UNITS],
+                    lhsT=hc_codes[s][:, nodes].bitcast(FP8X4),
+                    lhsT_scale=hc_scales[s][:, nodes],
                     rhs=ck_codes[:].bitcast(FP8X4),
                     rhs_scale=ck_scales[:],
                     start=True,
                     stop=True,
                 )
-            cand[q] = ending.tile([P, BANK], F32, name="cand", tag="cand")
-            nc.scalar.activation(out=cand[q][:], in_=pre[:], func=TANH)
+            cand[s] = ending.tile([P, BATCH * UNITS], F32, name="cand", tag="cand")
+            nc.scalar.activation(out=cand[s][:], in_=pre[:], func=TANH)
 
-        def blend_first(q):
-            diff[q] = ending.tile([P, BANK], F32, name="diff", tag="diff")
+        def blend(s):
+            q, j = divmod(s, ROWS)
+            rows = slice(q * ROUND, (q + 1) * ROUND)
+            fresh = ending.tile([P, BATCH * UNITS], F32)
+            nc.vector.scalar_tensor_tensor(
+                out=fresh[:].rearrange("p (b k) -> p b k", b=BATCH),
+                in0=u_raw[q][:].rearrange("p (b j k) -> p b j k", b=BATCH, j=ROWS)[:, :, j, :],
+                scalar=1.0,
+                in1=cand[s][:].rearrange("p (b k) -> p b k", b=BATCH),
+                op0=ALU.subtract,
+                op1=ALU.mult,
+            )
+            z = ending.tile([P, BATCH * UNITS], F32)
             nc.vector.tensor_tensor(
-                out=diff[q][:].rearrange("p (b j k) -> p b j k", b=BATCH, j=ROWS),
-                in0=prev_bank[q][:].bitcast(BF16).rearrange("p (b k j) -> p b j k", b=BATCH, j=ROWS),
-                in1=cand[q][:].rearrange("p (b j k) -> p b j k", b=BATCH, j=ROWS),
+                out=z[:].rearrange("p (b k) -> p b k", b=BATCH),
+                in0=kept[q][:].rearrange("p (b j k) -> p b j k", b=BATCH, j=ROWS)[:, :, j, :],
+                in1=fresh[:].rearrange("p (b k) -> p b k", b=BATCH),
                 op=ALU.subtract,
             )
-
-        def blend_last(q):
-            rows = slice(q * ROUND, (q + 1) * ROUND)
-            nc.vector.tensor_tensor(out=diff[q][:], in0=diff[q][:], in1=u_raw[q][:], op=ALU.mult)
-            z = ending.tile([P, BANK], F32)
-            nc.vector.tensor_tensor(out=z[:], in0=diff[q][:], in1=cand[q][:], op=ALU.add)
-            nc.gpsimd.dma_start(
-                out=out_rows[:, rows, :].rearrange("b (p j) k -> p b (j k)", j=ROWS),
-                in_=z[:].rearrange("p (b x) -> p b x", b=BATCH),
+            nc.sync.dma_start(
+                out=out_rows[:, rows, :].rearrange("b (p j) k -> p b j k", j=ROWS)[:, :, j, :],
+                in_=z[:].rearrange("p (b k) -> p b k", b=BATCH),
             )
 
-        for h in range(LEAD):
-            quantise_supports(h)
-        for h in range(HALF_STEPS):
-            q, stage = divmod(h, PER_ROUND)
-            s, half = divmod(h, HALVES)
-            if half == 0 and s > 0:
+        quantise_supports(0, both_engines)
+
+        ck_grouped = keep.tile([P, UNITS * PACK], BF16, align_bytes=64)
+        ck_codes = keep.tile([P, UNITS], U32, align_bytes=64)
+        ck_scales = keep.tile([P, UNITS], U8, align_bytes=64)
+        nc.vector.tensor_copy(
+            out=ck_grouped[:].rearrange("p (k t) -> p k t", t=PACK),
+            in_=ck_raw[:].rearrange("p (t k) -> p k t", t=PACK),
+        )
+        nc.vector.quantize_mx(out=ck_codes[:].bitcast(FP8X4), scales=ck_scales[:], in_=ck_grouped[:])
+
+        for s in range(STEPS + 3):
+            q, j = divmod(s, ROWS)
+            if 1 <= s <= STEPS:
                 collect(s - 1)
-            if q > 0 and stage == 0:
-                quantise_hc(q - 1)
-            if q > 0 and stage == 1:
-                transpose_state(q - 1)
-            if q > 0 and stage == 2:
-                blend_first(q - 1)
-            if q > 0 and stage == 3:
-                blend_last(q - 1)
-            if h + LEAD < HALF_STEPS:
-                quantise_supports(h + LEAD)
-            if half == 0:
+            if 3 <= s:
+                blend(s - 3)
+            if j == 0 and 1 <= q <= ROUNDS:
+                old_part(q - 1)
+            if s + 1 < STEPS:
+                quantise_supports(s + 1, scalar_only)
+            if s < STEPS:
                 features(s)
-            if q > 0 and stage == 1:
-                candidate(q - 1)
-            diffuse(h)
-            if stage == PER_ROUND - 1 - LEAD and q + AHEAD < ROUNDS:
-                load_round(q + AHEAD)
-        collect(STEPS - 1)
-        quantise_hc(ROUNDS - 1)
-        transpose_state(ROUNDS - 1)
-        candidate(ROUNDS - 1)
-        blend_first(ROUNDS - 1)
-        blend_last(ROUNDS - 1)
+            if 2 <= s <= STEPS + 1:
+                candidate(s - 2)
+            if s < STEPS:
+                diffuse(s)
+            if j == 0 and q + AHEAD <= ROUNDS:
+                fetch(q + AHEAD)

@@ -55,8 +55,8 @@ def tile_gcrnncell_pb_kernel(tc, r_prev, h_diff, u, state, support0, support1, c
         small_in = stack.enter_context(tc.tile_pool(name="small_in", bufs=AHEAD + 2))
         moving = stack.enter_context(tc.tile_pool(name="moving", bufs=6))
         ending = stack.enter_context(tc.tile_pool(name="ending", bufs=3))
-        banks = stack.enter_context(tc.psum_pool(name="banks", bufs=4))
-        sums = stack.enter_context(tc.psum_pool(name="sums", bufs=BATCH))
+        banks = stack.enter_context(tc.psum_pool(name="banks", bufs=3))
+        sums = stack.enter_context(tc.psum_pool(name="sums", bufs=4))
         single = stack.enter_context(tc.psum_pool(name="single", bufs=1))
         stack.enter_context(tc.manual_schedule())
 
@@ -141,55 +141,52 @@ def tile_gcrnncell_pb_kernel(tc, r_prev, h_diff, u, state, support0, support1, c
         kept = {}
         cand = {}
 
-        def quantise_supports(s, copies):
+        def quantise_supports(s, pair, copies):
             q, j = divmod(s, ROWS)
-            for pair in range(PASSES // PAIR):
-                grouped = moving.tile([P, PACK * BANK], BF16, align_bytes=64)
-                for i in range(SUPPORTS):
-                    first = (j * PASSES // PAIR + pair) * BANK
-                    transpose_512_words(
-                        nc,
-                        banks,
-                        ident_f32[:],
-                        copies[i],
-                        sup_raw[q, i][:].bitcast(F32)[:, first : first + BANK],
-                        grouped[:].bitcast(F32).rearrange("p (g i x) -> p g i x", g=PAIR, i=SUPPORTS)[:, :, i, :],
-                    )
-                sup_codes[s, pair] = moving.tile([P, BANK], U32, name="codes", tag="codes", align_bytes=64)
-                sup_scales[s, pair] = moving.tile([P, BANK], U8, name="scales", tag="scales", align_bytes=64)
-                nc.vector.quantize_mx(
-                    out=sup_codes[s, pair][:].bitcast(FP8X4), scales=sup_scales[s, pair][:], in_=grouped[:]
+            grouped = moving.tile([P, PACK * BANK], BF16, align_bytes=64)
+            for i in range(SUPPORTS):
+                first = (j * PASSES // PAIR + pair) * BANK
+                transpose_512_words(
+                    nc,
+                    banks,
+                    ident_f32[:],
+                    copies[i],
+                    sup_raw[q, i][:].bitcast(F32)[:, first : first + BANK],
+                    grouped[:].bitcast(F32).rearrange("p (g i x) -> p g i x", g=PAIR, i=SUPPORTS)[:, :, i, :],
+                )
+            sup_codes[s, pair] = moving.tile([P, BANK], U32, name="codes", tag="codes", align_bytes=64)
+            sup_scales[s, pair] = moving.tile([P, BANK], U8, name="scales", tag="scales", align_bytes=64)
+            nc.vector.quantize_mx(
+                out=sup_codes[s, pair][:].bitcast(FP8X4), scales=sup_scales[s, pair][:], in_=grouped[:]
+            )
+
+        def features(s, b):
+            q, j = divmod(s, ROWS)
+            planes[s, b] = sums.tile([P, BANK], F32, name="planes", tag="sum")
+            for t in range(FEATS // P):
+                first = (b * ROWS + j) * FEATS + t * P
+                nc.tensor.matmul(
+                    out=planes[s, b][:, t * P : (t + 1) * P],
+                    lhsT=h_raw[q][:, first : first + P],
+                    rhs=ident_bf16[:],
+                    start=True,
+                    stop=True,
                 )
 
-        def features(s):
-            q, j = divmod(s, ROWS)
-            for b in range(BATCH):
-                planes[s, b] = sums.tile([P, BANK], F32, name="planes", tag="planes")
-                for t in range(FEATS // P):
-                    first = (b * ROWS + j) * FEATS + t * P
-                    nc.tensor.matmul(
-                        out=planes[s, b][:, t * P : (t + 1) * P],
-                        lhsT=h_raw[q][:, first : first + P],
-                        rhs=ident_bf16[:],
-                        start=True,
-                        stop=True,
-                    )
-
-        def diffuse(s):
-            for g in range(PASSES):
-                pair, local = divmod(g, PAIR)
+        def diffuse(s, pair, b):
+            for local in range(PAIR):
+                g = pair * PAIR + local
                 nodes = slice(local * SUPPORTS * P, (local + 1) * SUPPORTS * P)
-                for b in range(BATCH):
-                    units = slice((b * PASSES + g) * UNITS, (b * PASSES + g + 1) * UNITS)
-                    nc.tensor.matmul_mx(
-                        out=planes[s, b][:, FEATS:BANK],
-                        lhsT=r_codes[:, units].bitcast(FP8X4),
-                        lhsT_scale=r_scales[:, units],
-                        rhs=sup_codes[s, pair][:, nodes].bitcast(FP8X4),
-                        rhs_scale=sup_scales[s, pair][:, nodes],
-                        start=(g == 0),
-                        stop=(g == PASSES - 1),
-                    )
+                units = slice((b * PASSES + g) * UNITS, (b * PASSES + g + 1) * UNITS)
+                nc.tensor.matmul_mx(
+                    out=planes[s, b][:, FEATS:BANK],
+                    lhsT=r_codes[:, units].bitcast(FP8X4),
+                    lhsT_scale=r_scales[:, units],
+                    rhs=sup_codes[s, pair][:, nodes].bitcast(FP8X4),
+                    rhs_scale=sup_scales[s, pair][:, nodes],
+                    start=(g == 0),
+                    stop=(g == PASSES - 1),
+                )
 
         def collect(s):
             hc_grouped = ending.tile([P, BATCH * P * PACK], BF16, align_bytes=64)
@@ -218,7 +215,7 @@ def tile_gcrnncell_pb_kernel(tc, r_prev, h_diff, u, state, support0, support1, c
             )
 
         def candidate(s):
-            pre = single.tile([P, BATCH * UNITS], F32)
+            pre = sums.tile([P, BATCH * UNITS], F32, name="pre", tag="sum")
             for b in range(BATCH):
                 nodes = slice(b * P, (b + 1) * P)
                 nc.tensor.matmul_mx(
@@ -257,7 +254,8 @@ def tile_gcrnncell_pb_kernel(tc, r_prev, h_diff, u, state, support0, support1, c
                 in_=z[:].rearrange("p (b k) -> p b k", b=BATCH),
             )
 
-        quantise_supports(0, both_engines)
+        for pair in range(PASSES // PAIR):
+            quantise_supports(0, pair, both_engines)
 
         ck_grouped = keep.tile([P, UNITS * PACK], BF16, align_bytes=64)
         ck_codes = keep.tile([P, UNITS], U32, align_bytes=64)
@@ -276,13 +274,15 @@ def tile_gcrnncell_pb_kernel(tc, r_prev, h_diff, u, state, support0, support1, c
                 blend(s - 3)
             if j == 0 and 1 <= q <= ROUNDS:
                 old_part(q - 1)
-            if s + 1 < STEPS:
-                quantise_supports(s + 1, scalar_only)
-            if s < STEPS:
-                features(s)
-            if 2 <= s <= STEPS + 1:
-                candidate(s - 2)
-            if s < STEPS:
-                diffuse(s)
+            for pair in range(PASSES // PAIR):
+                if s + 1 < STEPS:
+                    quantise_supports(s + 1, pair, scalar_only)
+                if pair == 1 and 2 <= s <= STEPS + 1:
+                    candidate(s - 2)
+                if s < STEPS:
+                    for b in range(BATCH):
+                        if pair == 0:
+                            features(s, b)
+                        diffuse(s, pair, b)
             if j == 0 and q + AHEAD <= ROUNDS:
                 fetch(q + AHEAD)

@@ -133,17 +133,21 @@ def tile_gcrnncell_pb_kernel(tc, r_prev, h_diff, u, state, support0, support1, c
             )
         nc.vector.quantize_mx(out=r_codes[:].bitcast(FP8X4), scales=r_scales[:], in_=r_grouped[:])
 
+        sup_grouped = {}
         sup_codes = {}
         sup_scales = {}
         planes = {}
+        hc_grouped = {}
         hc_codes = {}
         hc_scales = {}
         kept = {}
+        fresh = {}
         cand = {}
 
-        def quantise_supports(s, pair, copies):
+        def transpose_supports(s, pair, copies):
             q, j = divmod(s, ROWS)
-            grouped = moving.tile([P, PACK * BANK], BF16, align_bytes=64)
+            sup_grouped[s, pair] = moving.tile([P, PACK * BANK], BF16, name="grouped", tag="grouped", align_bytes=64)
+            grouped = sup_grouped[s, pair]
             for i in range(SUPPORTS):
                 first = (j * PASSES // PAIR + pair) * BANK
                 transpose_512_words(
@@ -154,10 +158,12 @@ def tile_gcrnncell_pb_kernel(tc, r_prev, h_diff, u, state, support0, support1, c
                     sup_raw[q, i][:].bitcast(F32)[:, first : first + BANK],
                     grouped[:].bitcast(F32).rearrange("p (g i x) -> p g i x", g=PAIR, i=SUPPORTS)[:, :, i, :],
                 )
+
+        def quantise_supports(s, pair):
             sup_codes[s, pair] = moving.tile([P, BANK], U32, name="codes", tag="codes", align_bytes=64)
             sup_scales[s, pair] = moving.tile([P, BANK], U8, name="scales", tag="scales", align_bytes=64)
             nc.vector.quantize_mx(
-                out=sup_codes[s, pair][:].bitcast(FP8X4), scales=sup_scales[s, pair][:], in_=grouped[:]
+                out=sup_codes[s, pair][:].bitcast(FP8X4), scales=sup_scales[s, pair][:], in_=sup_grouped[s, pair][:]
             )
 
         def features(s, b):
@@ -189,15 +195,17 @@ def tile_gcrnncell_pb_kernel(tc, r_prev, h_diff, u, state, support0, support1, c
                 )
 
         def collect(s):
-            hc_grouped = ending.tile([P, BATCH * P * PACK], BF16, align_bytes=64)
+            hc_grouped[s] = ending.tile([P, BATCH * P * PACK], BF16, name="hc", tag="hc", align_bytes=64)
             for b in range(BATCH):
                 both_engines[b](
-                    out=hc_grouped[:, b * P * PACK : (b + 1) * P * PACK].rearrange("p (m t) -> p m t", t=PACK),
+                    out=hc_grouped[s][:, b * P * PACK : (b + 1) * P * PACK].rearrange("p (m t) -> p m t", t=PACK),
                     in_=planes[s, b][:].rearrange("p (t m) -> p m t", t=PACK),
                 )
+
+        def quantise_hc(s):
             hc_codes[s] = ending.tile([P, BATCH * P], U32, name="hc_codes", tag="hc_codes", align_bytes=64)
             hc_scales[s] = ending.tile([P, BATCH * P], U8, name="hc_scales", tag="hc_scales", align_bytes=64)
-            nc.vector.quantize_mx(out=hc_codes[s][:].bitcast(FP8X4), scales=hc_scales[s][:], in_=hc_grouped[:])
+            nc.vector.quantize_mx(out=hc_codes[s][:].bitcast(FP8X4), scales=hc_scales[s][:], in_=hc_grouped[s][:])
 
         def old_part(q):
             prev_bank = single.tile([P, BATCH * UNITS], F32)
@@ -230,23 +238,26 @@ def tile_gcrnncell_pb_kernel(tc, r_prev, h_diff, u, state, support0, support1, c
             cand[s] = ending.tile([P, BATCH * UNITS], F32, name="cand", tag="cand")
             nc.scalar.activation(out=cand[s][:], in_=pre[:], func=TANH)
 
-        def blend(s):
+        def blend_first(s):
             q, j = divmod(s, ROWS)
-            rows = slice(q * ROUND, (q + 1) * ROUND)
-            fresh = ending.tile([P, BATCH * UNITS], F32)
+            fresh[s] = ending.tile([P, BATCH * UNITS], F32, name="fresh", tag="fresh")
             nc.vector.scalar_tensor_tensor(
-                out=fresh[:].rearrange("p (b k) -> p b k", b=BATCH),
+                out=fresh[s][:].rearrange("p (b k) -> p b k", b=BATCH),
                 in0=u_raw[q][:].rearrange("p (b j k) -> p b j k", b=BATCH, j=ROWS)[:, :, j, :],
                 scalar=1.0,
                 in1=cand[s][:].rearrange("p (b k) -> p b k", b=BATCH),
                 op0=ALU.subtract,
                 op1=ALU.mult,
             )
+
+        def blend_last(s):
+            q, j = divmod(s, ROWS)
+            rows = slice(q * ROUND, (q + 1) * ROUND)
             z = ending.tile([P, BATCH * UNITS], F32)
             nc.vector.tensor_tensor(
                 out=z[:].rearrange("p (b k) -> p b k", b=BATCH),
                 in0=kept[q][:].rearrange("p (b j k) -> p b j k", b=BATCH, j=ROWS)[:, :, j, :],
-                in1=fresh[:].rearrange("p (b k) -> p b k", b=BATCH),
+                in1=fresh[s][:].rearrange("p (b k) -> p b k", b=BATCH),
                 op=ALU.subtract,
             )
             nc.sync.dma_start(
@@ -255,7 +266,8 @@ def tile_gcrnncell_pb_kernel(tc, r_prev, h_diff, u, state, support0, support1, c
             )
 
         for pair in range(PASSES // PAIR):
-            quantise_supports(0, pair, both_engines)
+            transpose_supports(0, pair, both_engines)
+        quantise_supports(0, 0)
 
         ck_grouped = keep.tile([P, UNITS * PACK], BF16, align_bytes=64)
         ck_codes = keep.tile([P, UNITS], U32, align_bytes=64)
@@ -270,19 +282,29 @@ def tile_gcrnncell_pb_kernel(tc, r_prev, h_diff, u, state, support0, support1, c
             q, j = divmod(s, ROWS)
             if 1 <= s <= STEPS:
                 collect(s - 1)
+            if s < STEPS:
+                quantise_supports(s, 1)
             if 3 <= s:
-                blend(s - 3)
+                blend_first(s - 3)
+            if 1 <= s <= STEPS:
+                quantise_hc(s - 1)
+            if 3 <= s:
+                blend_last(s - 3)
             if j == 0 and 1 <= q <= ROUNDS:
                 old_part(q - 1)
-            for pair in range(PASSES // PAIR):
-                if s + 1 < STEPS:
-                    quantise_supports(s + 1, pair, scalar_only)
-                if pair == 1 and 2 <= s <= STEPS + 1:
-                    candidate(s - 2)
-                if s < STEPS:
-                    for b in range(BATCH):
-                        if pair == 0:
-                            features(s, b)
-                        diffuse(s, pair, b)
+            if s + 1 < STEPS:
+                transpose_supports(s + 1, 0, scalar_only)
+            if s < STEPS:
+                for b in range(BATCH):
+                    features(s, b)
+                    diffuse(s, 0, b)
+            if s + 1 < STEPS:
+                quantise_supports(s + 1, 0)
+                transpose_supports(s + 1, 1, scalar_only)
+            if 2 <= s <= STEPS + 1:
+                candidate(s - 2)
+            if s < STEPS:
+                for b in range(BATCH):
+                    diffuse(s, 1, b)
             if j == 0 and q + AHEAD <= ROUNDS:
                 fetch(q + AHEAD)

@@ -55,8 +55,8 @@ def tile_gcrnncell_pb_kernel(tc, r_prev, h_diff, u, state, support0, support1, c
         small_in = stack.enter_context(tc.tile_pool(name="small_in", bufs=AHEAD + 2))
         moving = stack.enter_context(tc.tile_pool(name="moving", bufs=6))
         ending = stack.enter_context(tc.tile_pool(name="ending", bufs=3))
-        banks = stack.enter_context(tc.psum_pool(name="banks", bufs=3))
-        sums = stack.enter_context(tc.psum_pool(name="sums", bufs=4))
+        banks = stack.enter_context(tc.psum_pool(name="banks", bufs=4))
+        sums = stack.enter_context(tc.psum_pool(name="sums", bufs=BATCH))
         single = stack.enter_context(tc.psum_pool(name="single", bufs=1))
         stack.enter_context(tc.manual_schedule())
 
@@ -168,7 +168,7 @@ def tile_gcrnncell_pb_kernel(tc, r_prev, h_diff, u, state, support0, support1, c
 
         def features(s, b):
             q, j = divmod(s, ROWS)
-            planes[s, b] = sums.tile([P, BANK], F32, name="planes", tag="sum")
+            planes[s, b] = sums.tile([P, BANK], F32, name="planes", tag="planes")
             for t in range(FEATS // P):
                 first = (b * ROWS + j) * FEATS + t * P
                 nc.tensor.matmul(
@@ -223,7 +223,7 @@ def tile_gcrnncell_pb_kernel(tc, r_prev, h_diff, u, state, support0, support1, c
             )
 
         def candidate(s):
-            pre = sums.tile([P, BATCH * UNITS], F32, name="pre", tag="sum")
+            pre = single.tile([P, BATCH * UNITS], F32)
             for b in range(BATCH):
                 nodes = slice(b * P, (b + 1) * P)
                 nc.tensor.matmul_mx(
@@ -293,18 +293,17 @@ def tile_gcrnncell_pb_kernel(tc, r_prev, h_diff, u, state, support0, support1, c
             if j == 0 and 1 <= q <= ROUNDS:
                 old_part(q - 1)
             if s + 1 < STEPS:
-                transpose_supports(s + 1, 0, scalar_only)
+                for pair in range(PASSES // PAIR):
+                    transpose_supports(s + 1, pair, scalar_only)
+                quantise_supports(s + 1, 0)
             if s < STEPS:
                 for b in range(BATCH):
                     features(s, b)
-                    diffuse(s, 0, b)
-            if s + 1 < STEPS:
-                quantise_supports(s + 1, 0)
-                transpose_supports(s + 1, 1, scalar_only)
             if 2 <= s <= STEPS + 1:
                 candidate(s - 2)
             if s < STEPS:
-                for b in range(BATCH):
-                    diffuse(s, 1, b)
+                for pair in range(PASSES // PAIR):
+                    for b in range(BATCH):
+                        diffuse(s, pair, b)
             if j == 0 and q + AHEAD <= ROUNDS:
                 fetch(q + AHEAD)

@@ -55,6 +55,7 @@ def tile_gcrnncell_pb_kernel(tc, r_prev, h_diff, u, state, support0, support1, c
         small_in = stack.enter_context(tc.tile_pool(name="small_in", bufs=AHEAD + 2))
         moving = stack.enter_context(tc.tile_pool(name="moving", bufs=6))
         ending = stack.enter_context(tc.tile_pool(name="ending", bufs=3))
+        results = stack.enter_context(tc.tile_pool(name="results", bufs=ROUNDS))
         banks = stack.enter_context(tc.psum_pool(name="banks", bufs=4))
         sums = stack.enter_context(tc.psum_pool(name="sums", bufs=BATCH))
         single = stack.enter_context(tc.psum_pool(name="single", bufs=1))
@@ -142,6 +143,7 @@ def tile_gcrnncell_pb_kernel(tc, r_prev, h_diff, u, state, support0, support1, c
         hc_scales = {}
         kept = {}
         fresh = {}
+        z = {}
         cand = {}
 
         def transpose_supports(s, pair, copies):
@@ -252,17 +254,20 @@ def tile_gcrnncell_pb_kernel(tc, r_prev, h_diff, u, state, support0, support1, c
 
         def blend_last(s):
             q, j = divmod(s, ROWS)
-            rows = slice(q * ROUND, (q + 1) * ROUND)
-            z = ending.tile([P, BATCH * UNITS], F32)
+            if j == 0:
+                z[q] = results.tile([P, BANK], F32, name="z", tag="z")
             nc.vector.tensor_tensor(
-                out=z[:].rearrange("p (b k) -> p b k", b=BATCH),
+                out=z[q][:].rearrange("p (b j k) -> p b j k", b=BATCH, j=ROWS)[:, :, j, :],
                 in0=kept[q][:].rearrange("p (b j k) -> p b j k", b=BATCH, j=ROWS)[:, :, j, :],
                 in1=fresh[s][:].rearrange("p (b k) -> p b k", b=BATCH),
                 op=ALU.subtract,
             )
+
+        def store(q):
+            rows = slice(q * ROUND, (q + 1) * ROUND)
             nc.sync.dma_start(
-                out=out_rows[:, rows, :].rearrange("b (p j) k -> p b j k", j=ROWS)[:, :, j, :],
-                in_=z[:].rearrange("p (b k) -> p b k", b=BATCH),
+                out=out_rows[:, rows, :].rearrange("b (p j) k -> p b (j k)", j=ROWS),
+                in_=z[q][:].rearrange("p (b x) -> p b x", b=BATCH),
             )
 
         for pair in range(PASSES // PAIR):
@@ -307,3 +312,6 @@ def tile_gcrnncell_pb_kernel(tc, r_prev, h_diff, u, state, support0, support1, c
                         diffuse(s, pair, b)
             if j == 0 and q + AHEAD <= ROUNDS:
                 fetch(q + AHEAD)
+            for done in range(ROUNDS):
+                if s == ROWS * max(done + 2, ROUNDS - AHEAD):
+                    store(done)

@@ -26,8 +26,22 @@ ROWS = 2
 ROUND = P * ROWS
 ROUNDS = NODES // ROUND
 STEPS = ROUNDS * ROWS
-AHEAD = 3
-FIRST_PIECES = 4
+STATE_ROUNDS = 2
+SMALL = 7
+ENDING = 3
+MOVING = 6
+AHEAD = 5
+ALT = True
+LAG = lambda t: 3
+OLD_AT = lambda x: x - 1 if x < 12 else x - 2
+OLD_FIRST = True
+COPIES = lambda s, pair, nc: (nc.scalar.copy, nc.scalar.copy)
+PB = lambda s: [(p, b) for p in range(2) for b in range(2)]
+EARLY = 0
+CKAT = 1
+STORE_FROM = 10
+TAIL = 2
+SWAP = ()
 
 FLOPS = 2 * SUPPORTS * BATCH * UNITS * NODES * NODES + 2 * BATCH * NODES * (FEATS + SUPPORTS * UNITS) * UNITS
 
@@ -52,9 +66,10 @@ def tile_gcrnncell_pb_kernel(tc, r_prev, h_diff, u, state, support0, support1, c
     with ExitStack() as stack:
         keep = stack.enter_context(tc.tile_pool(name="keep", bufs=1))
         big_in = stack.enter_context(tc.tile_pool(name="big_in", bufs=AHEAD))
-        small_in = stack.enter_context(tc.tile_pool(name="small_in", bufs=AHEAD + 2))
-        moving = stack.enter_context(tc.tile_pool(name="moving", bufs=6))
-        ending = stack.enter_context(tc.tile_pool(name="ending", bufs=3))
+        small_in = stack.enter_context(tc.tile_pool(name="small_in", bufs=SMALL))
+        states_in = stack.enter_context(tc.tile_pool(name="states_in", bufs=ROUNDS // STATE_ROUNDS))
+        moving = stack.enter_context(tc.tile_pool(name="moving", bufs=MOVING))
+        ending = stack.enter_context(tc.tile_pool(name="ending", bufs=ENDING))
         results = stack.enter_context(tc.tile_pool(name="results", bufs=ROUNDS))
         banks = stack.enter_context(tc.psum_pool(name="banks", bufs=4))
         sums = stack.enter_context(tc.psum_pool(name="sums", bufs=BATCH))
@@ -66,50 +81,98 @@ def tile_gcrnncell_pb_kernel(tc, r_prev, h_diff, u, state, support0, support1, c
         u_raw = {}
         state_raw = {}
 
-        def fetch(q):
-            if q < ROUNDS:
-                rows = slice(q * ROUND, (q + 1) * ROUND)
-                for i in range(SUPPORTS):
+        ck_raw = keep.tile([P, PACK * UNITS], BF16)
+        r_raw = keep.tile([P, BATCH * NODES], BF16)
+
+        def load_r(b, piece, pieces):
+            width = NODES // pieces
+            first = piece * width
+            nc.sync.dma_start(
+                out=r_raw[:, b * NODES + first : b * NODES + first + width], in_=r_prev[b, :, first : first + width]
+            )
+
+        def load_ck():
+            nc.sync.dma_start(
+                out=ck_raw[:].rearrange("p (t k) -> p t k", t=PACK), in_=c_kernel.rearrange("(t p) k -> p t k", p=P)
+            )
+
+        def load_supports(q, piece, pieces):
+            rows = slice(q * ROUND, (q + 1) * ROUND)
+            width = ROWS * NODES // pieces
+            cols = slice(piece * width, (piece + 1) * width)
+            for i in range(SUPPORTS):
+                if piece == 0:
                     sup_raw[q, i] = big_in.tile([P, ROWS * NODES], BF16, name="sup", tag="sup%d" % i)
-                pieces = max(1, FIRST_PIECES >> q)
-                width = ROWS * NODES // pieces
-                for piece in range(pieces):
-                    cols = slice(piece * width, (piece + 1) * width)
-                    for i in range(SUPPORTS):
-                        nc.sync.dma_start(
-                            out=sup_raw[q, i][:, cols],
-                            in_=supports[i][rows, :].rearrange("(p j) n -> p (j n)", j=ROWS)[:, cols],
-                        )
-                h_raw[q] = small_in.tile([P, BATCH * ROWS * FEATS], BF16, name="h", tag="h")
                 nc.sync.dma_start(
-                    out=h_raw[q][:].rearrange("p (b x) -> p b x", b=BATCH),
-                    in_=h_diff[:, rows, :].rearrange("b (p j) c -> p b (j c)", j=ROWS),
-                )
-            if q >= 1:
-                rows = slice((q - 1) * ROUND, q * ROUND)
-                state_raw[q - 1] = small_in.tile([P, BATCH * ROUND], BF16, name="st", tag="st")
-                nc.sync.dma_start(
-                    out=state_raw[q - 1][:].rearrange("p (b n) -> p b n", b=BATCH), in_=state_rows[:, :, rows]
-                )
-                u_raw[q - 1] = small_in.tile([P, BATCH * ROWS * UNITS], BF16, name="gate", tag="gate")
-                nc.sync.dma_start(
-                    out=u_raw[q - 1][:].rearrange("p (b x) -> p b x", b=BATCH),
-                    in_=u[:, rows, :].rearrange("b (p j) k -> p b (j k)", j=ROWS),
+                    out=sup_raw[q, i][:, cols],
+                    in_=supports[i][rows, :].rearrange("(p j) n -> p (j n)", j=ROWS)[:, cols],
                 )
 
-        r_raw = keep.tile([P, BATCH * NODES], BF16)
-        for b in range(BATCH):
-            for pair in range(PASSES // PAIR):
-                cols = slice(pair * PAIR * K_PASS, (pair + 1) * PAIR * K_PASS)
-                first = b * NODES + pair * PAIR * K_PASS
-                nc.sync.dma_start(out=r_raw[:, first : first + PAIR * K_PASS], in_=r_prev[b, :, cols])
-        fetch(0)
-        ck_raw = keep.tile([P, PACK * UNITS], BF16)
-        nc.sync.dma_start(
-            out=ck_raw[:].rearrange("p (t k) -> p t k", t=PACK), in_=c_kernel.rearrange("(t p) k -> p t k", p=P)
-        )
-        for q in range(1, AHEAD):
-            fetch(q)
+        def load_features(q):
+            rows = slice(q * ROUND, (q + 1) * ROUND)
+            h_raw[q] = small_in.tile([P, BATCH * ROWS * FEATS], BF16, name="h", tag="h")
+            nc.sync.dma_start(
+                out=h_raw[q][:].rearrange("p (b x) -> p b x", b=BATCH),
+                in_=h_diff[:, rows, :].rearrange("b (p j) c -> p b (j c)", j=ROWS),
+            )
+
+        def load_state(q):
+            rows = slice(q * ROUND, (q + STATE_ROUNDS) * ROUND)
+            state_raw[q // STATE_ROUNDS] = states_in.tile([P, BATCH * STATE_ROUNDS * ROUND], BF16, name="st", tag="st")
+            nc.sync.dma_start(
+                out=state_raw[q // STATE_ROUNDS][:].rearrange("p (b n) -> p b n", b=BATCH), in_=state_rows[:, :, rows]
+            )
+
+        def load_gate(q):
+            rows = slice(q * ROUND, (q + 1) * ROUND)
+            u_raw[q] = small_in.tile([P, BATCH * ROWS * UNITS], BF16, name="gate", tag="gate")
+            nc.sync.dma_start(
+                out=u_raw[q][:].rearrange("p (b x) -> p b x", b=BATCH),
+                in_=u[:, rows, :].rearrange("b (p j) k -> p b (j k)", j=ROWS),
+            )
+
+        def loads():
+            items = []
+            def at(q):
+                return -1 if q < AHEAD else (q - AHEAD) * ROWS
+            ends = []
+            for q in range(ROUNDS):
+                if q % STATE_ROUNDS == 0:
+                    ends.append((q, load_state, q))
+                ends.append((q, load_gate, q))
+            def rload():
+                for b in range(BATCH):
+                    for piece in range(1):
+                        items.append((-1, load_r, b, piece, 1))
+            PIECES = [2,2,2,1,1,1,1,1]
+            if 0 == 0:
+                rload()
+            lastq = 0
+            for q in range(ROUNDS):
+                pieces = PIECES[q]
+                for piece in range(pieces):
+                    items.append((at(q), load_supports, q, piece, pieces))
+                    if q == 0 and 0 == piece + 1:
+                        rload()
+                    if piece == (pieces - 1 if 1 else 0):
+                        items.append((at(q), load_features, q))
+                        if q == 0:
+                            items.append((at(q), load_ck))
+                while ends and ends[0][0] <= q - 1:
+                    e = ends.pop(0)
+                    items.append((at(q),) + e[1:])
+            for e in ends:
+                items.append((at(ROUNDS - 1),) + e[1:])
+            return items
+
+        queue = list(loads())
+
+        def issue(s):
+            while queue and queue[0][0] <= s:
+                item = queue.pop(0)
+                item[1](*item[2:])
+
+        issue(-1)
 
         ident_f32 = keep.tile([P, P], F32)
         make_identity(nc, ident_f32[:])
@@ -170,7 +233,10 @@ def tile_gcrnncell_pb_kernel(tc, r_prev, h_diff, u, state, support0, support1, c
 
         def features(s, b):
             q, j = divmod(s, ROWS)
-            planes[s, b] = sums.tile([P, BANK], F32, name="planes", tag="planes")
+            if s == STEPS - 1 and ALT:
+                planes[s, b] = banks.tile([P, BANK], F32, name="planes", tag="bank")
+            else:
+                planes[s, b] = sums.tile([P, BANK], F32, name="planes", tag="planes")
             for t in range(FEATS // P):
                 first = (b * ROWS + j) * FEATS + t * P
                 nc.tensor.matmul(
@@ -204,17 +270,25 @@ def tile_gcrnncell_pb_kernel(tc, r_prev, h_diff, u, state, support0, support1, c
                     in_=planes[s, b][:].rearrange("p (t m) -> p m t", t=PACK),
                 )
 
-        def quantise_hc(s):
+        def quantise_hc(s, parts):
             hc_codes[s] = ending.tile([P, BATCH * P], U32, name="hc_codes", tag="hc_codes", align_bytes=64)
             hc_scales[s] = ending.tile([P, BATCH * P], U8, name="hc_scales", tag="hc_scales", align_bytes=64)
-            nc.vector.quantize_mx(out=hc_codes[s][:].bitcast(FP8X4), scales=hc_scales[s][:], in_=hc_grouped[s][:])
+            for part in range(parts):
+                nodes = slice(part * BATCH * P // parts, (part + 1) * BATCH * P // parts)
+                nc.vector.quantize_mx(
+                    out=hc_codes[s][:, nodes].bitcast(FP8X4),
+                    scales=hc_scales[s][:, nodes],
+                    in_=hc_grouped[s][:, nodes.start * PACK : nodes.stop * PACK],
+                )
 
         def old_part(q):
             prev_bank = single.tile([P, BATCH * UNITS], F32)
             for b in range(BATCH):
-                cols = slice(b * P, (b + 1) * P)
+                first = (b * STATE_ROUNDS + q % STATE_ROUNDS) * P
                 nc.tensor.transpose(
-                    out=prev_bank[:, cols], in_=state_raw[q][:].bitcast(F32)[:, cols], identity=ident_f32[:]
+                    out=prev_bank[:, b * P : (b + 1) * P],
+                    in_=state_raw[q // STATE_ROUNDS][:].bitcast(F32)[:, first : first + P],
+                    identity=ident_f32[:],
                 )
             kept[q] = ending.tile([P, BANK], F32, name="kept", tag="kept")
             nc.vector.tensor_tensor(
@@ -224,7 +298,7 @@ def tile_gcrnncell_pb_kernel(tc, r_prev, h_diff, u, state, support0, support1, c
                 op=ALU.mult,
             )
 
-        def candidate(s):
+        def candidate(s, parts):
             pre = single.tile([P, BATCH * UNITS], F32)
             for b in range(BATCH):
                 nodes = slice(b * P, (b + 1) * P)
@@ -238,37 +312,45 @@ def tile_gcrnncell_pb_kernel(tc, r_prev, h_diff, u, state, support0, support1, c
                     stop=True,
                 )
             cand[s] = ending.tile([P, BATCH * UNITS], F32, name="cand", tag="cand")
-            nc.scalar.activation(out=cand[s][:], in_=pre[:], func=TANH)
+            for part in range(parts):
+                cols = slice(part * BATCH * UNITS // parts, (part + 1) * BATCH * UNITS // parts)
+                nc.scalar.activation(out=cand[s][:, cols], in_=pre[:, cols], func=TANH)
 
-        def blend_first(s):
+        def blend_first(s, parts):
             q, j = divmod(s, ROWS)
             fresh[s] = ending.tile([P, BATCH * UNITS], F32, name="fresh", tag="fresh")
-            nc.vector.scalar_tensor_tensor(
-                out=fresh[s][:].rearrange("p (b k) -> p b k", b=BATCH),
-                in0=u_raw[q][:].rearrange("p (b j k) -> p b j k", b=BATCH, j=ROWS)[:, :, j, :],
-                scalar=1.0,
-                in1=cand[s][:].rearrange("p (b k) -> p b k", b=BATCH),
-                op0=ALU.subtract,
-                op1=ALU.mult,
-            )
+            for part in range(parts):
+                bs = slice(part * BATCH // parts, (part + 1) * BATCH // parts)
+                nc.vector.scalar_tensor_tensor(
+                    out=fresh[s][:].rearrange("p (b k) -> p b k", b=BATCH)[:, bs],
+                    in0=u_raw[q][:].rearrange("p (b j k) -> p b j k", b=BATCH, j=ROWS)[:, bs, j, :],
+                    scalar=1.0,
+                    in1=cand[s][:].rearrange("p (b k) -> p b k", b=BATCH)[:, bs],
+                    op0=ALU.subtract,
+                    op1=ALU.mult,
+                )
 
-        def blend_last(s):
+        def blend_last(s, parts):
             q, j = divmod(s, ROWS)
             if j == 0:
                 z[q] = results.tile([P, BANK], F32, name="z", tag="z")
-            nc.vector.tensor_tensor(
-                out=z[q][:].rearrange("p (b j k) -> p b j k", b=BATCH, j=ROWS)[:, :, j, :],
-                in0=kept[q][:].rearrange("p (b j k) -> p b j k", b=BATCH, j=ROWS)[:, :, j, :],
-                in1=fresh[s][:].rearrange("p (b k) -> p b k", b=BATCH),
-                op=ALU.subtract,
-            )
+            for part in range(parts):
+                bs = slice(part * BATCH // parts, (part + 1) * BATCH // parts)
+                nc.vector.tensor_tensor(
+                    out=z[q][:].rearrange("p (b j k) -> p b j k", b=BATCH, j=ROWS)[:, bs, j, :],
+                    in0=kept[q][:].rearrange("p (b j k) -> p b j k", b=BATCH, j=ROWS)[:, bs, j, :],
+                    in1=fresh[s][:].rearrange("p (b k) -> p b k", b=BATCH)[:, bs],
+                    op=ALU.subtract,
+                )
 
-        def store(q):
+        def store(q, parts):
             rows = slice(q * ROUND, (q + 1) * ROUND)
-            nc.sync.dma_start(
-                out=out_rows[:, rows, :].rearrange("b (p j) k -> p b (j k)", j=ROWS),
-                in_=z[q][:].rearrange("p (b x) -> p b x", b=BATCH),
-            )
+            for part in range(parts):
+                bs = slice(part * BATCH // parts, (part + 1) * BATCH // parts)
+                nc.sync.dma_start(
+                    out=out_rows[bs, rows, :].rearrange("b (p j) k -> p b (j k)", j=ROWS),
+                    in_=z[q][:].rearrange("p (b x) -> p b x", b=BATCH)[:, bs],
+                )
 
         for pair in range(PASSES // PAIR):
             transpose_supports(0, pair, both_engines)
@@ -277,41 +359,69 @@ def tile_gcrnncell_pb_kernel(tc, r_prev, h_diff, u, state, support0, support1, c
         ck_grouped = keep.tile([P, UNITS * PACK], BF16, align_bytes=64)
         ck_codes = keep.tile([P, UNITS], U32, align_bytes=64)
         ck_scales = keep.tile([P, UNITS], U8, align_bytes=64)
-        nc.vector.tensor_copy(
-            out=ck_grouped[:].rearrange("p (k t) -> p k t", t=PACK),
-            in_=ck_raw[:].rearrange("p (t k) -> p k t", t=PACK),
-        )
-        nc.vector.quantize_mx(out=ck_codes[:].bitcast(FP8X4), scales=ck_scales[:], in_=ck_grouped[:])
+        def ck_work():
+            nc.vector.tensor_copy(
+                out=ck_grouped[:].rearrange("p (k t) -> p k t", t=PACK),
+                in_=ck_raw[:].rearrange("p (t k) -> p k t", t=PACK),
+            )
+            nc.vector.quantize_mx(out=ck_codes[:].bitcast(FP8X4), scales=ck_scales[:], in_=ck_grouped[:])
 
+
+        def blend_at(t):
+            return t + LAG(t)
+
+        stored = []
         for s in range(STEPS + 3):
             q, j = divmod(s, ROWS)
+            due = [t for t in range(STEPS) if blend_at(t) == s]
+
+            def olds():
+                for r in range(ROUNDS):
+                    if OLD_AT(blend_at(ROWS * r)) == s:
+                        old_part(r)
+
+            def run():
+                if s + 1 < STEPS:
+                    for pair in range(PASSES // PAIR):
+                        transpose_supports(s + 1, pair, COPIES(s, pair, nc))
+            def multiply():
+                if s < STEPS:
+                    for pair, b in (PB(s)):
+                        diffuse(s, pair, b)
+            if s in SWAP:
+                quantise_supports(s, 1)
             if 1 <= s <= STEPS:
                 collect(s - 1)
-            if s < STEPS:
+            if s < STEPS and s not in SWAP:
                 quantise_supports(s, 1)
-            if 3 <= s:
-                blend_first(s - 3)
+            for t in due:
+                blend_first(t, TAIL if t == STEPS - 1 else 1)
             if 1 <= s <= STEPS:
-                quantise_hc(s - 1)
-            if 3 <= s:
-                blend_last(s - 3)
-            if j == 0 and 1 <= q <= ROUNDS:
-                old_part(q - 1)
+                quantise_hc(s - 1, TAIL if s == STEPS else 1)
+            for t in due:
+                blend_last(t, TAIL if t == STEPS - 1 else 1)
+            if OLD_FIRST:
+                olds()
+            if s < EARLY:
+                for b in range(BATCH):
+                    features(s, b)
+                multiply()
+            run()
+            if not OLD_FIRST:
+                olds()
             if s + 1 < STEPS:
-                for pair in range(PASSES // PAIR):
-                    transpose_supports(s + 1, pair, scalar_only)
                 quantise_supports(s + 1, 0)
-            if s < STEPS:
+            if s == CKAT:
+                ck_work()
+            if EARLY <= s < STEPS:
                 for b in range(BATCH):
                     features(s, b)
             if 2 <= s <= STEPS + 1:
-                candidate(s - 2)
-            if s < STEPS:
-                for pair in range(PASSES // PAIR):
-                    for b in range(BATCH):
-                        diffuse(s, pair, b)
-            if j == 0 and q + AHEAD <= ROUNDS:
-                fetch(q + AHEAD)
+                candidate(s - 2, TAIL if s == STEPS + 1 else 1)
+            if s >= EARLY:
+                multiply()
+            issue(s)
             for done in range(ROUNDS):
-                if s == ROWS * max(done + 2, ROUNDS - AHEAD):
-                    store(done)
+                if done not in stored and s >= STORE_FROM and s >= blend_at(ROWS * done + 1):
+                    store(done, TAIL if done == ROUNDS - 1 else 1)
+                    stored.append(done)

@@ -28,20 +28,21 @@ ROUNDS = NODES // ROUND
 STEPS = ROUNDS * ROWS
 STATE_ROUNDS = 2
 SMALL = 7
-ENDING = 3
+ENDING = 4
 MOVING = 6
 AHEAD = 5
 ALT = True
-LAG = lambda t: 3
-OLD_AT = lambda x: x - 1 if x < 12 else x - 2
-OLD_FIRST = True
+LAG = lambda t: 4 if t == 14 else 3
+OLD_AT = lambda x: x - 1
+OLD_FIRST = lambda s: False
 COPIES = lambda s, pair, nc: (nc.scalar.copy, nc.scalar.copy)
 PB = lambda s: [(p, b) for p in range(2) for b in range(2)]
 EARLY = 0
 CKAT = 1
 STORE_FROM = 10
 TAIL = 2
-SWAP = ()
+SWAP = (15,)
+KEND = True
 
 FLOPS = 2 * SUPPORTS * BATCH * UNITS * NODES * NODES + 2 * BATCH * NODES * (FEATS + SUPPORTS * UNITS) * UNITS
 
@@ -144,7 +145,7 @@ def tile_gcrnncell_pb_kernel(tc, r_prev, h_diff, u, state, support0, support1, c
                 for b in range(BATCH):
                     for piece in range(1):
                         items.append((-1, load_r, b, piece, 1))
-            PIECES = [2,2,2,1,1,1,1,1]
+            PIECES = [2,2,2,2,1,1,1,1]
             if 0 == 0:
                 rload()
             lastq = 0
@@ -205,6 +206,7 @@ def tile_gcrnncell_pb_kernel(tc, r_prev, h_diff, u, state, support0, support1, c
         hc_codes = {}
         hc_scales = {}
         kept = {}
+        prev_bank = {}
         fresh = {}
         z = {}
         cand = {}
@@ -282,18 +284,20 @@ def tile_gcrnncell_pb_kernel(tc, r_prev, h_diff, u, state, support0, support1, c
                 )
 
         def old_part(q):
-            prev_bank = single.tile([P, BATCH * UNITS], F32)
+            prev_bank[q] = single.tile([P, BATCH * UNITS], F32, name="prev", tag="prev")
             for b in range(BATCH):
                 first = (b * STATE_ROUNDS + q % STATE_ROUNDS) * P
                 nc.tensor.transpose(
-                    out=prev_bank[:, b * P : (b + 1) * P],
+                    out=prev_bank[q][:, b * P : (b + 1) * P],
                     in_=state_raw[q // STATE_ROUNDS][:].bitcast(F32)[:, first : first + P],
                     identity=ident_f32[:],
                 )
+
+        def keep_old(q):
             kept[q] = ending.tile([P, BANK], F32, name="kept", tag="kept")
             nc.vector.tensor_tensor(
                 out=kept[q][:].rearrange("p (b j k) -> p b j k", b=BATCH, j=ROWS),
-                in0=prev_bank[:].bitcast(BF16).rearrange("p (b k j) -> p b j k", b=BATCH, j=ROWS),
+                in0=prev_bank[q][:].bitcast(BF16).rearrange("p (b k j) -> p b j k", b=BATCH, j=ROWS),
                 in1=u_raw[q][:].rearrange("p (b j k) -> p b j k", b=BATCH, j=ROWS),
                 op=ALU.mult,
             )
@@ -375,10 +379,16 @@ def tile_gcrnncell_pb_kernel(tc, r_prev, h_diff, u, state, support0, support1, c
             q, j = divmod(s, ROWS)
             due = [t for t in range(STEPS) if blend_at(t) == s]
 
+            ends = []
+
             def olds():
                 for r in range(ROUNDS):
                     if OLD_AT(blend_at(ROWS * r)) == s:
                         old_part(r)
+                        if KEND:
+                            ends.append(r)
+                        else:
+                            keep_old(r)
 
             def run():
                 if s + 1 < STEPS:
@@ -400,17 +410,19 @@ def tile_gcrnncell_pb_kernel(tc, r_prev, h_diff, u, state, support0, support1, c
                 quantise_hc(s - 1, TAIL if s == STEPS else 1)
             for t in due:
                 blend_last(t, TAIL if t == STEPS - 1 else 1)
-            if OLD_FIRST:
+            if OLD_FIRST(s):
                 olds()
             if s < EARLY:
                 for b in range(BATCH):
                     features(s, b)
                 multiply()
             run()
-            if not OLD_FIRST:
+            if not OLD_FIRST(s):
                 olds()
             if s + 1 < STEPS:
                 quantise_supports(s + 1, 0)
+            for r in ends:
+                keep_old(r)
             if s == CKAT:
                 ck_work()
             if EARLY <= s < STEPS:

@@ -145,7 +145,7 @@ def tile_gcrnncell_pb_kernel(tc, r_prev, h_diff, u, state, support0, support1, c
                 for b in range(BATCH):
                     for piece in range(1):
                         items.append((-1, load_r, b, piece, 1))
-            PIECES = [2,2,2,2,1,1,1,1]
+            PIECES = [2,2,2,2,2,2,2,2]
             if 0 == 0:
                 rload()
             lastq = 0

@@ -214,16 +214,23 @@ def tile_gcrnncell_pb_kernel(tc, r_prev, h_diff, u, state, support0, support1, c
         def transpose_supports(s, pair, copies):
             q, j = divmod(s, ROWS)
             sup_grouped[s, pair] = moving.tile([P, PACK * BANK], BF16, name="grouped", tag="grouped", align_bytes=64)
-            grouped = sup_grouped[s, pair]
-            for i in range(SUPPORTS):
-                first = (j * PASSES // PAIR + pair) * BANK
-                transpose_512_words(
-                    nc,
-                    banks,
-                    ident_f32[:],
-                    copies[i],
-                    sup_raw[q, i][:].bitcast(F32)[:, first : first + BANK],
-                    grouped[:].bitcast(F32).rearrange("p (g i x) -> p g i x", g=PAIR, i=SUPPORTS)[:, :, i, :],
+            for local in range(PAIR):
+                first = (j * PASSES + pair * PAIR + local) * K_PASS // 2
+                bank = banks.tile([P, BANK], F32, name="bank", tag="bank")
+                for i in range(SUPPORTS):
+                    for half in range(2):
+                        block = i * 2 + half
+                        words = slice(first + half * P, first + (half + 1) * P)
+                        nc.tensor.transpose(
+                            out=bank[:, block * P : (block + 1) * P],
+                            in_=sup_raw[q, i][:].bitcast(F32)[:, words],
+                            identity=ident_f32[:],
+                        )
+                copies[local](
+                    out=sup_grouped[s, pair][:]
+                    .bitcast(F32)
+                    .rearrange("p (g i r u) -> p g i r u", g=PAIR, i=SUPPORTS, u=2)[:, local],
+                    in_=bank[:].rearrange("p (i u r) -> p i r u", i=SUPPORTS, u=2),
                 )
 
         def quantise_supports(s, pair):

@@ -43,6 +43,8 @@ STORE_FROM = 10
 TAIL = 2
 SWAP = (15,)
 KEND = True
+QFIRST = False
+CB = lambda s: s % 4 != 3
 
 FLOPS = 2 * SUPPORTS * BATCH * UNITS * NODES * NODES + 2 * BATCH * NODES * (FEATS + SUPPORTS * UNITS) * UNITS
 
@@ -274,7 +276,7 @@ def tile_gcrnncell_pb_kernel(tc, r_prev, h_diff, u, state, support0, support1, c
         def collect(s):
             hc_grouped[s] = ending.tile([P, BATCH * P * PACK], BF16, name="hc", tag="hc", align_bytes=64)
             for b in range(BATCH):
-                both_engines[b](
+                both_engines[b if CB(s) else 0](
                     out=hc_grouped[s][:, b * P * PACK : (b + 1) * P * PACK].rearrange("p (m t) -> p m t", t=PACK),
                     in_=planes[s, b][:].rearrange("p (t m) -> p m t", t=PACK),
                 )
@@ -411,9 +413,11 @@ def tile_gcrnncell_pb_kernel(tc, r_prev, h_diff, u, state, support0, support1, c
                 collect(s - 1)
             if s < STEPS and s not in SWAP:
                 quantise_supports(s, 1)
+            if s == STEPS and QFIRST:
+                quantise_hc(s - 1, TAIL)
             for t in due:
                 blend_first(t, TAIL if t == STEPS - 1 else 1)
-            if 1 <= s <= STEPS:
+            if 1 <= s <= STEPS and not (s == STEPS and QFIRST):
                 quantise_hc(s - 1, TAIL if s == STEPS else 1)
             for t in due:
                 blend_last(t, TAIL if t == STEPS - 1 else 1)

from contextlib import ExitStack

import concourse.mybir as mybir
from concourse.masks import make_identity

F32 = mybir.dt.float32
BF16 = mybir.dt.bfloat16
U32 = mybir.dt.uint32
U8 = mybir.dt.uint8
FP8X4 = mybir.dt.float8_e4m3fn_x4
ALU = mybir.AluOpType
TANH = mybir.ActivationFunctionType.Tanh

P = 128
BATCH = 2
NODES = 2048
UNITS = 128
FEATS = 256
SUPPORTS = 2
PACK = 4
K_PASS = P * PACK
PASSES = NODES // K_PASS
BANK = 512
PAIR = 2
ROWS = 2
ROUND = P * ROWS
ROUNDS = NODES // ROUND
STEPS = ROUNDS * ROWS
STATE_ROUNDS = 2
SMALL = 7
ENDING = 4
MOVING = 6
AHEAD = 5
ALT = True
LAG = lambda t: 4 if t == 14 else 3
OLD_AT = lambda x: x - 1
OLD_FIRST = lambda s: False
COPIES = lambda s, pair, nc: (nc.scalar.copy, nc.scalar.copy)
PB = lambda s: [(p, b) for p in range(2) for b in range(2)]
EARLY = 0
CKAT = 1
STORE_FROM = 10
TAIL = 2
SWAP = (15,)
KEND = True
QFIRST = False
CB = lambda s: s % 4 != 3

FLOPS = 2 * SUPPORTS * BATCH * UNITS * NODES * NODES + 2 * BATCH * NODES * (FEATS + SUPPORTS * UNITS) * UNITS


def transpose_512_words(nc, banks, identity, copy, words_in, words_out):
    bank = banks.tile([P, BANK], F32, tag="bank")
    for block in range(BANK // P):
        cols = slice(block * P, (block + 1) * P)
        nc.tensor.transpose(out=bank[:, cols], in_=words_in[:, cols], identity=identity)
    copy(
        out=words_out.rearrange("p g (r u) -> p g r u", u=2),
        in_=bank[:].rearrange("p (g u r) -> p g r u", g=PAIR, u=2),
    )


def tile_gcrnncell_pb_kernel(tc, r_prev, h_diff, u, state, support0, support1, c_kernel, out):
    nc = tc.nc
    supports = (support0, support1)
    state_rows = state.rearrange("b (k n) -> k b n", n=NODES)
    out_rows = out.rearrange("b (m k) -> b m k", k=UNITS)

    with ExitStack() as stack:
        keep = stack.enter_context(tc.tile_pool(name="keep", bufs=1))
        big_in = stack.enter_context(tc.tile_pool(name="big_in", bufs=AHEAD))
        small_in = stack.enter_context(tc.tile_pool(name="small_in", bufs=SMALL))
        states_in = stack.enter_context(tc.tile_pool(name="states_in", bufs=ROUNDS // STATE_ROUNDS))
        moving = stack.enter_context(tc.tile_pool(name="moving", bufs=MOVING))
        ending = stack.enter_context(tc.tile_pool(name="ending", bufs=ENDING))
        results = stack.enter_context(tc.tile_pool(name="results", bufs=ROUNDS))
        banks = stack.enter_context(tc.psum_pool(name="banks", bufs=4))
        sums = stack.enter_context(tc.psum_pool(name="sums", bufs=BATCH))
        single = stack.enter_context(tc.psum_pool(name="single", bufs=1))
        stack.enter_context(tc.manual_schedule())

        sup_raw = {}
        h_raw = {}
        u_raw = {}
        state_raw = {}

        ck_raw = keep.tile([P, PACK * UNITS], BF16)
        r_raw = keep.tile([P, BATCH * NODES], BF16)

        def load_r(b, piece, pieces):
            width = NODES // pieces
            first = piece * width
            nc.sync.dma_start(
                out=r_raw[:, b * NODES + first : b * NODES + first + width], in_=r_prev[b, :, first : first + width]
            )

        def load_ck():
            nc.sync.dma_start(
                out=ck_raw[:].rearrange("p (t k) -> p t k", t=PACK), in_=c_kernel.rearrange("(t p) k -> p t k", p=P)
            )

        def load_supports(q, piece, pieces):
            rows = slice(q * ROUND, (q + 1) * ROUND)
            width = ROWS * NODES // pieces
            cols = slice(piece * width, (piece + 1) * width)
            for i in range(SUPPORTS):
                if piece == 0:
                    sup_raw[q, i] = big_in.tile([P, ROWS * NODES], BF16, name="sup", tag="sup%d" % i)
                nc.sync.dma_start(
                    out=sup_raw[q, i][:, cols],
                    in_=supports[i][rows, :].rearrange("(p j) n -> p (j n)", j=ROWS)[:, cols],
                )

        def load_features(q):
            rows = slice(q * ROUND, (q + 1) * ROUND)
            h_raw[q] = small_in.tile([P, BATCH * ROWS * FEATS], BF16, name="h", tag="h")
            nc.sync.dma_start(
                out=h_raw[q][:].rearrange("p (b x) -> p b x", b=BATCH),
                in_=h_diff[:, rows, :].rearrange("b (p j) c -> p b (j c)", j=ROWS),
            )

        def load_state(q):
            rows = slice(q * ROUND, (q + STATE_ROUNDS) * ROUND)
            state_raw[q // STATE_ROUNDS] = states_in.tile([P, BATCH * STATE_ROUNDS * ROUND], BF16, name="st", tag="st")
            nc.sync.dma_start(
                out=state_raw[q // STATE_ROUNDS][:].rearrange("p (b n) -> p b n", b=BATCH), in_=state_rows[:, :, rows]
            )

        def load_gate(q):
            rows = slice(q * ROUND, (q + 1) * ROUND)
            u_raw[q] = small_in.tile([P, BATCH * ROWS * UNITS], BF16, name="gate", tag="gate")
            nc.sync.dma_start(
                out=u_raw[q][:].rearrange("p (b x) -> p b x", b=BATCH),
                in_=u[:, rows, :].rearrange("b (p j) k -> p b (j k)", j=ROWS),
            )

        def loads():
            items = []
            def at(q):
                return -1 if q < AHEAD else (q - AHEAD) * ROWS
            ends = []
            for q in range(ROUNDS):
                if q % STATE_ROUNDS == 0:
                    ends.append((q, load_state, q))
                ends.append((q, load_gate, q))
            def rload():
                for b in range(BATCH):
                    for piece in range(1):
                        items.append((-1, load_r, b, piece, 1))
            PIECES = [2,2,2,2,2,2,2,2]
            if 0 == 0:
                rload()
            lastq = 0
            for q in range(ROUNDS):
                pieces = PIECES[q]
                for piece in range(pieces):
                    items.append((at(q), load_supports, q, piece, pieces))
                    if q == 0 and 0 == piece + 1:
                        rload()
                    if piece == (pieces - 1 if 1 else 0):
                        items.append((at(q), load_features, q))
                        if q == 0:
                            items.append((at(q), load_ck))
                while ends and ends[0][0] <= q - 1:
                    e = ends.pop(0)
                    items.append((at(q),) + e[1:])
            for e in ends:
                items.append((at(ROUNDS - 1),) + e[1:])
            return items

        queue = list(loads())

        def issue(s):
            while queue and queue[0][0] <= s:
                item = queue.pop(0)
                item[1](*item[2:])

        issue(-1)

        ident_f32 = keep.tile([P, P], F32)
        make_identity(nc, ident_f32[:])
        ident_bf16 = keep.tile([P, P], BF16)
        make_identity(nc, ident_bf16[:])

        both_engines = (nc.scalar.copy, nc.vector.tensor_copy)
        scalar_only = (nc.scalar.copy, nc.scalar.copy)

        r_grouped = keep.tile([P, BATCH * NODES], BF16, align_bytes=64)
        r_codes = keep.tile([P, BATCH * PASSES * UNITS], U32, align_bytes=64)
        r_scales = keep.tile([P, BATCH * PASSES * UNITS], U8, align_bytes=64)
        for piece in range(BATCH * PASSES // PAIR):
            words = slice(piece * BANK, (piece + 1) * BANK)
            transpose_512_words(
                nc,
                banks,
                ident_f32[:],
                both_engines[piece % 2],
                r_raw[:].bitcast(F32)[:, words],
                r_grouped[:].bitcast(F32)[:, words].rearrange("p (g x) -> p g x", g=PAIR),
            )
        nc.vector.quantize_mx(out=r_codes[:].bitcast(FP8X4), scales=r_scales[:], in_=r_grouped[:])

        sup_grouped = {}
        sup_codes = {}
        sup_scales = {}
        planes = {}
        hc_grouped = {}
        hc_codes = {}
        hc_scales = {}
        kept = {}
        prev_bank = {}
        fresh = {}
        z = {}
        cand = {}

        def transpose_supports(s, pair, copies):
            q, j = divmod(s, ROWS)
            sup_grouped[s, pair] = moving.tile([P, PACK * BANK], BF16, name="grouped", tag="grouped", align_bytes=64)
            for local in range(PAIR):
                first = (j * PASSES + pair * PAIR + local) * K_PASS // 2
                bank = banks.tile([P, BANK], F32, name="bank", tag="bank")
                for i in range(SUPPORTS):
                    for half in range(2):
                        block = i * 2 + half
                        words = slice(first + half * P, first + (half + 1) * P)
                        nc.tensor.transpose(
                            out=bank[:, block * P : (block + 1) * P],
                            in_=sup_raw[q, i][:].bitcast(F32)[:, words],
                            identity=ident_f32[:],
                        )
                copies[local](
                    out=sup_grouped[s, pair][:]
                    .bitcast(F32)
                    .rearrange("p (g i r u) -> p g i r u", g=PAIR, i=SUPPORTS, u=2)[:, local],
                    in_=bank[:].rearrange("p (i u r) -> p i r u", i=SUPPORTS, u=2),
                )

        def quantise_supports(s, pair):
            sup_codes[s, pair] = moving.tile([P, BANK], U32, name="codes", tag="codes", align_bytes=64)
            sup_scales[s, pair] = moving.tile([P, BANK], U8, name="scales", tag="scales", align_bytes=64)
            nc.vector.quantize_mx(
                out=sup_codes[s, pair][:].bitcast(FP8X4), scales=sup_scales[s, pair][:], in_=sup_grouped[s, pair][:]
            )

        def features(s, b):
            q, j = divmod(s, ROWS)
            if s == STEPS - 1 and ALT:
                planes[s, b] = banks.tile([P, BANK], F32, name="planes", tag="bank")
            else:
                planes[s, b] = sums.tile([P, BANK], F32, name="planes", tag="planes")
            for t in range(FEATS // P):
                first = (b * ROWS + j) * FEATS + t * P
                nc.tensor.matmul(
                    out=planes[s, b][:, t * P : (t + 1) * P],
                    lhsT=h_raw[q][:, first : first + P],
                    rhs=ident_bf16[:],
                    start=True,
                    stop=True,
                )

        def diffuse(s, pair, b):
            for local in range(PAIR):
                g = pair * PAIR + local
                nodes = slice(local * SUPPORTS * P, (local + 1) * SUPPORTS * P)
                units = slice((b * PASSES + g) * UNITS, (b * PASSES + g + 1) * UNITS)
                nc.tensor.matmul_mx(
                    out=planes[s, b][:, FEATS:BANK],
                    lhsT=r_codes[:, units].bitcast(FP8X4),
                    lhsT_scale=r_scales[:, units],
                    rhs=sup_codes[s, pair][:, nodes].bitcast(FP8X4),
                    rhs_scale=sup_scales[s, pair][:, nodes],
                    start=(g == 0),
                    stop=(g == PASSES - 1),
                )

        def collect(s):
            hc_grouped[s] = ending.tile([P, BATCH * P * PACK], BF16, name="hc", tag="hc", align_bytes=64)
            for b in range(BATCH):
                both_engines[b if CB(s) else 0](
                    out=hc_grouped[s][:, b * P * PACK : (b + 1) * P * PACK].rearrange("p (m t) -> p m t", t=PACK),
                    in_=planes[s, b][:].rearrange("p (t m) -> p m t", t=PACK),
                )

        def quantise_hc(s, parts):
            hc_codes[s] = ending.tile([P, BATCH * P], U32, name="hc_codes", tag="hc_codes", align_bytes=64)
            hc_scales[s] = ending.tile([P, BATCH * P], U8, name="hc_scales", tag="hc_scales", align_bytes=64)
            for part in range(parts):
                nodes = slice(part * BATCH * P // parts, (part + 1) * BATCH * P // parts)
                nc.vector.quantize_mx(
                    out=hc_codes[s][:, nodes].bitcast(FP8X4),
                    scales=hc_scales[s][:, nodes],
                    in_=hc_grouped[s][:, nodes.start * PACK : nodes.stop * PACK],
                )

        def old_part(q):
            prev_bank[q] = single.tile([P, BATCH * UNITS], F32, name="prev", tag="prev")
            for b in range(BATCH):
                first = (b * STATE_ROUNDS + q % STATE_ROUNDS) * P
                nc.tensor.transpose(
                    out=prev_bank[q][:, b * P : (b + 1) * P],
                    in_=state_raw[q // STATE_ROUNDS][:].bitcast(F32)[:, first : first + P],
                    identity=ident_f32[:],
                )

        def keep_old(q):
            kept[q] = ending.tile([P, BANK], F32, name="kept", tag="kept")
            nc.vector.tensor_tensor(
                out=kept[q][:].rearrange("p (b j k) -> p b j k", b=BATCH, j=ROWS),
                in0=prev_bank[q][:].bitcast(BF16).rearrange("p (b k j) -> p b j k", b=BATCH, j=ROWS),
                in1=u_raw[q][:].rearrange("p (b j k) -> p b j k", b=BATCH, j=ROWS),
                op=ALU.mult,
            )

        def candidate(s, parts):
            pre = single.tile([P, BATCH * UNITS], F32)
            for b in range(BATCH):
                nodes = slice(b * P, (b + 1) * P)
                nc.tensor.matmul_mx(
                    out=pre[:, b * UNITS : (b + 1) * UNITS],
                    lhsT=hc_codes[s][:, nodes].bitcast(FP8X4),
                    lhsT_scale=hc_scales[s][:, nodes],
                    rhs=ck_codes[:].bitcast(FP8X4),
                    rhs_scale=ck_scales[:],
                    start=True,
                    stop=True,
                )
            cand[s] = ending.tile([P, BATCH * UNITS], F32, name="cand", tag="cand")
            for part in range(parts):
                cols = slice(part * BATCH * UNITS // parts, (part + 1) * BATCH * UNITS // parts)
                nc.scalar.activation(out=cand[s][:, cols], in_=pre[:, cols], func=TANH)

        def blend_first(s, parts):
            q, j = divmod(s, ROWS)
            fresh[s] = ending.tile([P, BATCH * UNITS], F32, name="fresh", tag="fresh")
            for part in range(parts):
                bs = slice(part * BATCH // parts, (part + 1) * BATCH // parts)
                nc.vector.scalar_tensor_tensor(
                    out=fresh[s][:].rearrange("p (b k) -> p b k", b=BATCH)[:, bs],
                    in0=u_raw[q][:].rearrange("p (b j k) -> p b j k", b=BATCH, j=ROWS)[:, bs, j, :],
                    scalar=1.0,
                    in1=cand[s][:].rearrange("p (b k) -> p b k", b=BATCH)[:, bs],
                    op0=ALU.subtract,
                    op1=ALU.mult,
                )

        def blend_last(s, parts):
            q, j = divmod(s, ROWS)
            if j == 0:
                z[q] = results.tile([P, BANK], F32, name="z", tag="z")
            for part in range(parts):
                bs = slice(part * BATCH // parts, (part + 1) * BATCH // parts)
                nc.vector.tensor_tensor(
                    out=z[q][:].rearrange("p (b j k) -> p b j k", b=BATCH, j=ROWS)[:, bs, j, :],
                    in0=kept[q][:].rearrange("p (b j k) -> p b j k", b=BATCH, j=ROWS)[:, bs, j, :],
                    in1=fresh[s][:].rearrange("p (b k) -> p b k", b=BATCH)[:, bs],
                    op=ALU.subtract,
                )

        def store(q, parts):
            rows = slice(q * ROUND, (q + 1) * ROUND)
            for part in range(parts):
                bs = slice(part * BATCH // parts, (part + 1) * BATCH // parts)
                nc.sync.dma_start(
                    out=out_rows[bs, rows, :].rearrange("b (p j) k -> p b (j k)", j=ROWS),
                    in_=z[q][:].rearrange("p (b x) -> p b x", b=BATCH)[:, bs],
                )

        for pair in range(PASSES // PAIR):
            transpose_supports(0, pair, both_engines)
        quantise_supports(0, 0)

        ck_grouped = keep.tile([P, UNITS * PACK], BF16, align_bytes=64)
        ck_codes = keep.tile([P, UNITS], U32, align_bytes=64)
        ck_scales = keep.tile([P, UNITS], U8, align_bytes=64)
        def ck_work():
            nc.vector.tensor_copy(
                out=ck_grouped[:].rearrange("p (k t) -> p k t", t=PACK),
                in_=ck_raw[:].rearrange("p (t k) -> p k t", t=PACK),
            )
            nc.vector.quantize_mx(out=ck_codes[:].bitcast(FP8X4), scales=ck_scales[:], in_=ck_grouped[:])


        def blend_at(t):
            return t + LAG(t)

        stored = []
        for s in range(STEPS + 3):
            q, j = divmod(s, ROWS)
            due = [t for t in range(STEPS) if blend_at(t) == s]

            ends = []

            def olds():
                for r in range(ROUNDS):
                    if OLD_AT(blend_at(ROWS * r)) == s:
                        old_part(r)
                        if KEND:
                            ends.append(r)
                        else:
                            keep_old(r)

            def run():
                if s + 1 < STEPS:
                    for pair in range(PASSES // PAIR):
                        transpose_supports(s + 1, pair, COPIES(s, pair, nc))
            def multiply():
                if s < STEPS:
                    for pair, b in (PB(s)):
                        diffuse(s, pair, b)
            if s in SWAP:
                quantise_supports(s, 1)
            if 1 <= s <= STEPS:
                collect(s - 1)
            if s < STEPS and s not in SWAP:
                quantise_supports(s, 1)
            if s == STEPS and QFIRST:
                quantise_hc(s - 1, TAIL)
            for t in due:
                blend_first(t, TAIL if t == STEPS - 1 else 1)
            if 1 <= s <= STEPS and not (s == STEPS and QFIRST):
                quantise_hc(s - 1, TAIL if s == STEPS else 1)
            for t in due:
                blend_last(t, TAIL if t == STEPS - 1 else 1)
            if OLD_FIRST(s):
                olds()
            if s < EARLY:
                for b in range(BATCH):
                    features(s, b)
                multiply()
            run()
            if not OLD_FIRST(s):
                olds()
            if s + 1 < STEPS:
                quantise_supports(s + 1, 0)
            for r in ends:
                keep_old(r)
            if s == CKAT:
                ck_work()
            if EARLY <= s < STEPS:
                for b in range(BATCH):
                    features(s, b)
            if 2 <= s <= STEPS + 1:
                candidate(s - 2, TAIL if s == STEPS + 1 else 1)
            if s >= EARLY:
                multiply()
            issue(s)
            for done in range(ROUNDS):
                if done not in stored and s >= STORE_FROM and s >= blend_at(ROWS * done + 1):
                    store(done, TAIL if done == ROUNDS - 1 else 1)
                    stored.append(done)
